import numpy as np
import ml_dtypes


def mxq(x, axis, fmt="e4m3"):
    dtype, down = {"e4m3": (ml_dtypes.float8_e4m3fn, 7), "e5m2": (ml_dtypes.float8_e5m2, 14)}[fmt]
    v = np.moveaxis(np.asarray(x, np.float32).astype(ml_dtypes.bfloat16).astype(np.float64), axis, -1)
    blocks = v.reshape(v.shape[:-1] + (-1, 32))
    amax = np.abs(blocks).max(-1, keepdims=True)
    byte = np.maximum(np.where(amax > 0, np.frexp(amax)[1] - 1 + 127, 0) - down, 1)
    scale = np.exp2(byte - 127.0)
    codes = (blocks / scale).astype(np.float32).astype(dtype).astype(np.float64)
    return np.moveaxis((codes * scale).reshape(v.shape), -1, axis)


WIDE = False


def mx_kscale(k):
    if not WIDE:
        return np.ones(k)
    levels = np.array([10, -10, 5, -5, 0])
    if k % 512:
        return np.exp2(np.random.permutation(np.resize(levels, k // 32))).repeat(32)
    a = np.empty((k // 512, 16))
    for p in range(k // 512):
        a[p, :8] = np.random.permutation(np.resize(levels, 8))
        for g in range(8):
            far = levels[np.abs(levels - a[p, g]) >= 10]
            a[p, g + 8] = far[np.random.randint(len(far))]
    return np.exp2(a.ravel()).repeat(32)


BF16 = ml_dtypes.bfloat16


def bf(x):
    return np.asarray(x, np.float32).astype(BF16)


def f64(x):
    return np.asarray(x).astype(np.float64)


E2M1 = np.array([0.0, 0.5, 1.0, 1.5, 2.0, 3.0, 4.0, 6.0, -0.0, -0.5, -1.0, -1.5, -2.0, -3.0, -4.0, -6.0])


def pack_weight(w, fmt):
    k, n = w.shape
    w = f64(bf(w)).reshape(k // 32, 32, n)
    amax = np.abs(w).max(1)
    if fmt == "e4m3":
        byte = np.frexp(amax)[1] - 1 + 127 - 7
    else:
        mant, ex = np.frexp(amax / 6.0)
        byte = np.where(mant > 0.5, ex, ex - 1) + 127
    byte = np.clip(np.where(amax > 0, byte, 1), 1, 254)
    scaled = (w * np.exp2(127.0 - byte)[:, None, :]).reshape(k, n).astype(np.float32)
    by_word = np.ascontiguousarray(scaled.reshape(k // 512, 128, 4, n).transpose(0, 1, 3, 2))
    if fmt == "e4m3":
        words = by_word.astype(ml_dtypes.float8_e4m3fn).view(np.uint8)
    else:
        c = by_word.astype(ml_dtypes.float4_e2m1fn).view(np.uint8) & 0xF
        words = c[..., 0::2] | (c[..., 1::2] << 4)
    return np.ascontiguousarray(words), np.ascontiguousarray(byte.astype(np.uint8).reshape(k // 512, 16, n))


def unpack_weight(words, scales, fmt):
    g, p, n, _ = words.shape
    if fmt == "e4m3":
        vals = np.ascontiguousarray(words).view(ml_dtypes.float8_e4m3fn).astype(np.float64)
    else:
        nib = np.empty((g, p, n, 4), np.uint8)
        nib[..., 0::2] = words & 0xF
        nib[..., 1::2] = words >> 4
        vals = E2M1[nib]
    vals = vals * np.repeat(np.exp2(scales.astype(np.float64) - 127.0), 8, axis=1)[..., None]
    return vals.transpose(0, 1, 3, 2).reshape(g * 512, n)


B, S, HID, NH, NKV, LORA, D_ROPE, D_NOPE, D_V = 2, 256, 2048, 16, 4, 512, 64, 128, 128
D_QK = D_NOPE + D_ROPE
ROPE_BASE = 10000.0


def rope(x):
    inv_freq = 1.0 / (ROPE_BASE ** (f64(np.arange(0, D_ROPE, 2)) / D_ROPE))
    freqs = np.outer(f64(np.arange(S)), inv_freq)
    emb = np.concatenate([freqs, freqs], axis=-1)
    cos = np.cos(emb)[None, :, None, :]
    sin = np.sin(emb)[None, :, None, :]
    x1, x2 = np.split(x, 2, axis=-1)
    rot = np.concatenate([-x2, x1], axis=-1)
    return x * cos + rot * sin


def draw0():
    s, t = mx_kscale(HID), mx_kscale(LORA)
    col = np.concatenate([np.ones(NH * D_QK), t])
    hidden_states = bf(np.random.standard_normal((B, S, HID)) * s)
    Wqkv_words, Wqkv_scales = pack_weight(np.random.standard_normal((HID, NH * D_QK + LORA)) / np.sqrt(HID) / s[:, None] * col, "e4m3")
    Wk_up_words, Wk_up_scales = pack_weight(np.random.standard_normal((LORA, NKV * D_QK)) / np.sqrt(LORA) / t[:, None], "e4m3")
    Wv_up_words, Wv_up_scales = pack_weight(np.random.standard_normal((LORA, NKV * D_V)) / np.sqrt(LORA) / t[:, None], "e4m3")
    return {
        "hidden_states": hidden_states,
        "Wqkv_words": Wqkv_words,
        "Wqkv_scales": Wqkv_scales,
        "Wk_up_words": Wk_up_words,
        "Wk_up_scales": Wk_up_scales,
        "Wv_up_words": Wv_up_words,
        "Wv_up_scales": Wv_up_scales,
    }


def core(hidden_states, Wqkv_words, Wqkv_scales, Wk_up_words, Wk_up_scales, Wv_up_words, Wv_up_scales):
    qkv = mxq(f64(hidden_states), 2, "e4m3") @ unpack_weight(Wqkv_words, Wqkv_scales, "e4m3")
    q, c_kv = np.split(qkv, [NH * D_QK], axis=-1)
    q = q.reshape(B, S, NH, D_QK)
    cq = mxq(c_kv, 2, "e4m3")
    k = (cq @ unpack_weight(Wk_up_words, Wk_up_scales, "e4m3")).reshape(B, S, NKV, D_QK)
    v = (cq @ unpack_weight(Wv_up_words, Wv_up_scales, "e4m3")).reshape(B, S, NKV, D_V)
    q_nope, q_rope = np.split(q, [D_NOPE], axis=-1)
    k_nope, k_rope = np.split(k, [D_NOPE], axis=-1)
    q = np.concatenate([q_nope, rope(q_rope)], axis=-1)
    k = np.concatenate([k_nope, rope(k_rope)], axis=-1)
    return q, k, v


def e4m3fn_bytes(y):
    return np.clip(np.asarray(y, np.float64), -448.0, 448.0).astype(np.float32).astype(ml_dtypes.float8_e4m3fn).view(np.uint8)


def e4m3fn_values(b):
    return np.asarray(b, np.uint8).view(ml_dtypes.float8_e4m3fn).astype(np.float64)


def setup_inputs():
    d = draw0()
    x0 = np.asarray(d['hidden_states']).astype(np.float64)
    s = (np.max(np.abs(x0), axis=(0, 1), keepdims=True) / 448.0).astype(np.float32)
    out = {}
    for k, v in d.items():
        if k == 'hidden_states':
            out['hidden_states_bytes'] = e4m3fn_bytes(x0 / s.astype(np.float64))
            out['hidden_states_scale'] = s
        else:
            out[k] = v
    return out


def reference(hidden_states_bytes, hidden_states_scale, Wqkv_words, Wqkv_scales, Wk_up_words, Wk_up_scales, Wv_up_words, Wv_up_scales):
    return core(e4m3fn_values(hidden_states_bytes) * hidden_states_scale.astype(np.float64), Wqkv_words, Wqkv_scales, Wk_up_words, Wk_up_scales, Wv_up_words, Wv_up_scales)

@@ -1,0 +1,477 @@
+import math
+from contextlib import ExitStack
+
+import concourse.mybir as mybir
+from concourse.masks import make_identity
+
+B, S, HID = 2, 256, 2048
+NH, NKV, LORA = 16, 4, 512
+D_NOPE, D_ROPE, D_V = 128, 64, 128
+D_QK = D_NOPE + D_ROPE
+NQ = NH * D_QK
+NK = NKV * D_QK
+NV = NKV * D_V
+TOK = B * S
+
+FLOPS = 2 * TOK * HID * (NQ + LORA) + 2 * TOK * LORA * (NK + NV)
+
+F32 = mybir.dt.float32
+BF16 = mybir.dt.bfloat16
+I32 = mybir.dt.int32
+U32 = mybir.dt.uint32
+U8 = mybir.dt.uint8
+FP8 = mybir.dt.float8_e4m3fn
+FP8X4 = mybir.dt.float8_e4m3fn_x4
+ALU = mybir.AluOpType
+ACT = mybir.ActivationFunctionType
+
+P = 128
+GROUPS = HID // 512
+BLK = 512
+HALF = 3 * BLK
+TILES = TOK // P
+
+
+def tile_multiheadlatentattentionwithgqafused_pa_w8_kernel(
+    tc,
+    x_bytes,
+    x_scale,
+    wqkv_words,
+    wqkv_scales,
+    wk_words,
+    wk_scales,
+    wv_words,
+    wv_scales,
+    out_q,
+    out_k,
+    out_v,
+):
+    nc = tc.nc
+    with ExitStack() as ctx:
+        keep = ctx.enter_context(tc.tile_pool(name="keep", bufs=1))
+        ring = ctx.enter_context(tc.tile_pool(name="ring", bufs=3))
+        ps_t = ctx.enter_context(tc.psum_pool(name="ps_t", bufs=2))
+        ps_a = ctx.enter_context(tc.psum_pool(name="ps_a", bufs=6))
+        ctx.enter_context(tc.manual_schedule())
+
+        x_rows = x_bytes.rearrange("b s k -> (b s) k")
+        q_rows = out_q.rearrange("b s h d -> (b s) (h d)")
+        k_rows = out_k.rearrange("b s h d -> (b s) (h d)")
+        v_rows = out_v.rearrange("b s h d -> (b s) (h d)")
+        wqkv = wqkv_words.rearrange("g p n t -> p g (n t)")
+
+        ident = keep.tile([P, P], F32, name="ident")
+        xb_first = keep.tile([P, 2, 512], U8, name="xb_first")
+        xb_rest = keep.tile([P, 2, 1536], U8, name="xb_rest")
+        xb_pair1 = keep.tile([P, 2, 2048], U8, name="xb_pair1")
+        xw_first = keep.tile([P, 2, 512], BF16, name="xw_first")
+        xw_rest = keep.tile([P, 2, 1536], BF16, name="xw_rest")
+        xw_pair1 = keep.tile([P, 2, 2048], BF16, name="xw_pair1")
+        xsc = keep.tile([P, GROUPS, 2, 2], F32, name="xsc")
+        xq = keep.tile([P, GROUPS, TOK], U32, name="xq", align_bytes=64)
+        xs = keep.tile([P, GROUPS, TOK], U8, name="xs", align_bytes=64)
+        wsc = keep.tile([P, NQ + LORA], U8, name="wsc", align_bytes=64)
+        upsc = keep.tile([P, NK + NV], U8, name="upsc", align_bytes=64)
+        w01 = [keep.tile([P, 2 * BLK], U32, name=f"w01_{g}", align_bytes=64) for g in range(GROUPS)]
+        wblk = {b: keep.tile([P, GROUPS, BLK], U32, name=f"w_{b}", align_bytes=64) for b in (2, 3, 4, 5)}
+        wlat_in = keep.tile([P, GROUPS, LORA], U32, name="wlat_in", align_bytes=64)
+        wlat = keep.tile([P, GROUPS, LORA], U32, name="wlat", align_bytes=64)
+        wlsc = keep.tile([P, LORA], U8, name="wlsc", align_bytes=64)
+        wk = keep.tile([P, NK], U32, name="wk", align_bytes=64)
+        wv = keep.tile([P, NV], U32, name="wv", align_bytes=64)
+        ckq = keep.tile([P, TOK], U32, name="ckq", align_bytes=64)
+        cks = keep.tile([P, TOK], U8, name="cks", align_bytes=64)
+        tab = keep.tile([P, 2, 2, D_ROPE], F32, name="tab")
+        q_out = {(i, h): keep.tile([P, HALF], F32, name=f"q_{i}_{h}") for i in range(TILES) for h in range(2)}
+        k_out = [keep.tile([P, NK], F32, name=f"k_{i}") for i in range(TILES)]
+        v_out = [keep.tile([P, NV], F32, name=f"v_{i}") for i in range(TILES)]
+
+        nc.vector.memset(wsc[:, 0 : 2 * BLK].bitcast(I32), 0)
+        nc.vector.memset(wsc[:, 2 * BLK :].bitcast(I32), 0)
+        nc.vector.memset(upsc[:].bitcast(I32), 0)
+        warm = keep.tile([P, 1], F32, name="warm")
+        nc.vector.memset(warm[:], 0.0)
+        warm_out = keep.tile([P, 1], F32, name="warm_out")
+        nc.scalar.dma_start(out=xsc[:], in_=x_scale.rearrange("a b (g p u e) -> p (a b g) u e", p=P, u=2, e=2))
+        nc.scalar.activation(out=warm_out[:], in_=warm[:], func=ACT.Sin)
+
+        make_identity(nc, ident[:])
+        pos = keep.tile([P, 2, 1], F32, name="pos")
+        nc.gpsimd.iota(pos[:], [[P, 2], [0, 1]], base=0, channel_multiplier=1, allow_small_or_imprecise_dtypes=True)
+        ang = keep.tile([P, 2, 2, 32], F32, name="ang")
+        nc.gpsimd.tensor_scalar(
+            out=ang[:, 0, :, 0:1], in0=pos[:], scalar1=1.0 / (2.0 * math.pi), scalar2=None, op0=ALU.mult
+        )
+        for m in (1, 2, 4, 8, 16):
+            nc.gpsimd.tensor_scalar(
+                out=ang[:, 0, :, m : 2 * m],
+                in0=ang[:, 0, :, 0:m],
+                scalar1=10000.0 ** (-m / 32.0),
+                scalar2=None,
+                op0=ALU.mult,
+            )
+        nc.gpsimd.tensor_scalar(out=ang[:, 1], in0=ang[:, 0], scalar1=0.25, scalar2=None, op0=ALU.add)
+
+        def load_x(pair, tile, k0, k1):
+            rows = x_rows[256 * pair : 256 * pair + 256, k0:k1]
+            nc.sync.dma_start(out=tile[:], in_=rows.rearrange("(j p) k -> p j k", p=P))
+
+        def load_scales(c0, c1):
+            for quad in range(4):
+                nc.sync.dma_start(
+                    out=wsc[32 * quad : 32 * quad + 16, c0:c1].bitcast(I32),
+                    in_=wqkv_scales[:, 4 * quad : 4 * quad + 4, c0:c1].bitcast(I32),
+                )
+
+        def load_block(tile, c0):
+            nc.sync.dma_start(
+                out=tile[:].bitcast(I32), in_=wqkv[:, :, 4 * c0 : 4 * (c0 + BLK)].bitcast(I32)
+            )
+
+        def load_w01(g):
+            nc.sync.dma_start(out=w01[g][:].bitcast(I32), in_=wqkv[:, g, 0 : 8 * BLK].bitcast(I32))
+
+        load_x(0, xb_first, 0, 512)
+        load_scales(0, 2 * BLK)
+        load_x(0, xb_rest, 512, 2048)
+        for g in range(GROUPS):
+            load_w01(g)
+        load_x(1, xb_pair1, 0, 2048)
+        load_block(wblk[2], 2 * BLK)
+        load_scales(2 * BLK, NQ + LORA)
+        load_block(wblk[3], 3 * BLK)
+        load_block(wblk[4], 4 * BLK)
+        load_block(wlat_in, NQ)
+        load_block(wblk[5], 5 * BLK)
+        for quad in range(4):
+            rows = slice(32 * quad, 32 * quad + 4)
+            nc.sync.dma_start(
+                out=upsc[rows, 0:NK].bitcast(I32), in_=wk_scales[0, 4 * quad : 4 * quad + 4, :].bitcast(I32)
+            )
+            nc.sync.dma_start(
+                out=upsc[rows, NK:].bitcast(I32), in_=wv_scales[0, 4 * quad : 4 * quad + 4, :].bitcast(I32)
+            )
+        nc.sync.dma_start(out=wk[:].bitcast(I32), in_=wk_words[0].rearrange("p n t -> p (n t)").bitcast(I32))
+        nc.sync.dma_start(out=wv[:].bitcast(I32), in_=wv_words[0].rearrange("p n t -> p (n t)").bitcast(I32))
+
+        def x_slices(pair, j, g):
+            if pair == 1:
+                return xb_pair1[:, j, 512 * g : 512 * g + 512], xw_pair1[:, j, 512 * g : 512 * g + 512]
+            if g == 0:
+                return xb_first[:, j, :], xw_first[:, j, :]
+            return xb_rest[:, j, 512 * (g - 1) : 512 * g], xw_rest[:, j, 512 * (g - 1) : 512 * g]
+
+        def widen(pair, g):
+            for j in range(2):
+                src, dst = x_slices(pair, j, g)
+                nc.scalar.copy(out=dst, in_=src.bitcast(FP8))
+
+        turned = {}
+
+        def turn(pair, g):
+            bank = ps_t.tile([P, 2, 2, P], F32, name="bank", tag="bank")
+            for j in range(2):
+                words = x_slices(pair, j, g)[1].bitcast(F32)
+                for u in range(2):
+                    nc.tensor.transpose(bank[:, j, u, :], words[:, u:256:2], ident[:])
+            turned[pair, g] = bank
+
+        def scale_quantize(pair, g):
+            bank = turned[pair, g]
+            parts = []
+            for j in range(2):
+                xt = ring.tile([P, P, 2, 2], BF16, name="xt", tag="xt", bufs=4, align_bytes=64)
+                src = bank[:, j].rearrange("p u r -> p (u r)").bitcast(BF16)
+                nc.vector.tensor_tensor(
+                    out=xt[:],
+                    in0=src.rearrange("p (u r e) -> p r u e", u=2, e=2),
+                    in1=xsc[:, g].unsqueeze(1).broadcast_to([P, P, 2, 2]),
+                    op=ALU.mult,
+                )
+                parts.append(xt)
+            for j in range(2):
+                cols = slice(256 * pair + 128 * j, 256 * pair + 128 * j + 128)
+                nc.vector.quantize_mx(
+                    out=xq[:, g, cols].bitcast(FP8X4),
+                    scales=xs[:, g, cols],
+                    in_=parts[j][:].rearrange("p r u e -> p (r u e)"),
+                )
+
+        acc = {}
+
+        def w_slice(b, g):
+            if b < 2:
+                return w01[g][:, BLK * b : BLK * b + BLK]
+            return wblk[b][:, g, :]
+
+        def q_pass(i, b, g):
+            if g == 0:
+                acc[i, b] = ps_a.tile([P, BLK], F32, name="acc", tag="acc")
+            rows = slice(P * i, P * i + P)
+            nc.tensor.matmul_mx(
+                out=acc[i, b][:],
+                lhsT=xq[:, g, rows].bitcast(FP8X4),
+                lhsT_scale=xs[:, g, rows],
+                rhs=w_slice(b, g).bitcast(FP8X4),
+                rhs_scale=wsc[4 * g : P, BLK * b : BLK * b + BLK],
+                start=(g == 0),
+                stop=(g == GROUPS - 1),
+            )
+
+        def q_group(i, b):
+            for g in range(GROUPS):
+                q_pass(i, b, g)
+
+        def heads(ap):
+            return ap.rearrange("p (h d) -> p h d", d=D_ROPE)
+
+        def rope(i, bank, dst, n):
+            prod = ring.tile([P, 2, 3, D_ROPE], F32, name="prod", tag="prod")
+            a = i % 2
+            nc.vector.tensor_tensor(
+                out=prod[:, :, 0:n, :],
+                in0=bank.unsqueeze(1).broadcast_to([P, 2, n, D_ROPE]),
+                in1=tab[:, a].unsqueeze(2).broadcast_to([P, 2, n, D_ROPE]),
+                op=ALU.mult,
+            )
+            nc.vector.tensor_tensor(
+                out=dst.rearrange("p h (k d) -> p h k d", k=2),
+                in0=prod[:, 0, 0:n, :].rearrange("p h (k d) -> p h k d", k=2),
+                in1=prod[:, 1, 0:n, :].rearrange("p h (k d) -> p h k d", k=2)[:, :, ::-1, :],
+                op=ALU.add,
+            )
+
+        def plain(bank, dst, first, lone):
+            for view in (bank, dst):
+                assert view.shape[1] == 8
+            pairs = slice(first, first + 6)
+            nc.scalar.copy(
+                out=dst[:, pairs, :].rearrange("p (a c) d -> p a c d", c=3)[:, :, 0:2, :],
+                in_=bank[:, pairs, :].rearrange("p (a c) d -> p a c d", c=3)[:, :, 0:2, :],
+            )
+            nc.scalar.copy(out=dst[:, lone, :], in_=bank[:, lone, :])
+
+        LAYOUT = ((2, 0, slice(6, 8)), (0, 1, slice(7, 8)), (1, 2, slice(0, 1)))
+
+        def finish_512(i, bank, dst, kind):
+            r0, first, lone = LAYOUT[kind]
+            src, to = heads(bank), heads(dst)
+            n = len(range(r0, 8, 3))
+            rope(i, src[:, r0:8:3, :], to[:, r0:8:3, :], n)
+            plain(src, to, first, lone)
+
+        def q_finish(i, b):
+            c0 = BLK * (b % 3)
+            finish_512(i, acc[i, b][:], q_out[i, b // 3][:, c0 : c0 + BLK], b % 3)
+
+        def q_store(i, h):
+            nc.sync.dma_start(out=q_rows[P * i : P * i + P, HALF * h : HALF * h + HALF], in_=q_out[i, h][:])
+
+        def q_store_block(i, b):
+            c0 = BLK * (b % 3)
+            nc.sync.dma_start(
+                out=q_rows[P * i : P * i + P, BLK * b : BLK * b + BLK], in_=q_out[i, b // 3][:, c0 : c0 + BLK]
+            )
+
+        def permute_latent():
+            nc.vector.tensor_copy(
+                out=wlat[:].bitcast(I32).rearrange("p g (t m) -> p g t m", t=4),
+                in_=wlat_in[:].bitcast(I32).rearrange("p g (m t) -> p g t m", t=4),
+            )
+            nc.vector.tensor_copy(
+                out=wlsc[:].rearrange("p (t m) -> p t m", t=4),
+                in_=wsc[:, NQ:].rearrange("p (m t) -> p t m", t=4),
+            )
+
+        def latent(i):
+            bank = ps_a.tile([P, BLK], F32, name="acc", tag="acc")
+            acc["lat", i] = bank
+            rows = slice(P * i, P * i + P)
+            for t in range(4):
+                cols = slice(P * t, P * t + P)
+                for g in range(GROUPS):
+                    nc.tensor.matmul_mx(
+                        out=bank[:, cols],
+                        lhsT=wlat[:, g, cols].bitcast(FP8X4),
+                        lhsT_scale=wlsc[4 * g : P, cols],
+                        rhs=xq[:, g, rows].bitcast(FP8X4),
+                        rhs_scale=xs[:, g, rows],
+                        start=(g == 0),
+                        stop=(g == GROUPS - 1),
+                    )
+
+        ck_tiles = {}
+
+        def latent_copy(i):
+            ck = ring.tile([P, P, 4], BF16, name="ck", tag="ck", bufs=2, align_bytes=64)
+            nc.scalar.copy(out=ck[:], in_=acc["lat", i][:].rearrange("p (t r) -> p r t", t=4))
+            ck_tiles[i] = ck
+
+        def latent_quantize(i):
+            rows = slice(P * i, P * i + P)
+            nc.vector.quantize_mx(
+                out=ckq[:, rows].bitcast(FP8X4),
+                scales=cks[:, rows],
+                in_=ck_tiles[i][:].rearrange("p r t -> p (r t)"),
+            )
+
+        def up(i, key, words, c0, n, s0):
+            bank = ps_a.tile([P, BLK], F32, name="acc", tag="acc")
+            acc[key, i] = bank
+            rows = slice(P * i, P * i + P)
+            nc.tensor.matmul_mx(
+                out=bank[:, 0:n],
+                lhsT=ckq[:, rows].bitcast(FP8X4),
+                lhsT_scale=cks[:, rows],
+                rhs=words[:, c0 : c0 + n].bitcast(FP8X4),
+                rhs_scale=upsc[:, s0 : s0 + n],
+                start=True,
+                stop=True,
+            )
+
+        def k_up(i):
+            up(i, "k0", wk, 0, 512, 0)
+            up(i, "k1", wk, 512, 256, 512)
+
+        def k_finish(i):
+            finish_512(i, acc["k0", i][:], k_out[i][:, 0:512], 0)
+            src = heads(acc["k1", i][:, 0:256])
+            to = heads(k_out[i][:, 512:768])
+            rope(i, src[:, 0:4:3, :], to[:, 0:4:3, :], 2)
+            nc.scalar.copy(out=to[:, 1:3, :], in_=src[:, 1:3, :])
+            nc.sync.dma_start(out=k_rows[P * i : P * i + P, :], in_=k_out[i][:])
+
+        def v_finish(i):
+            nc.scalar.copy(out=v_out[i][:], in_=acc["v", i][:])
+            nc.sync.dma_start(out=v_rows[P * i : P * i + P, :], in_=v_out[i][:])
+
+        def tables():
+            whole = keep.tile([P, 2, 2, 32], I32, name="whole")
+            nc.vector.tensor_copy(out=whole[:], in_=ang[:])
+            turns = keep.tile([P, 2, 2, 32], F32, name="turns")
+            nc.vector.tensor_copy(out=turns[:], in_=whole[:])
+            frac = keep.tile([P, 2, 2, 32], F32, name="frac")
+            nc.vector.tensor_tensor(out=frac[:], in0=ang[:], in1=turns[:], op=ALU.subtract)
+            two_pi = 2.0 * math.pi
+            nc.scalar.activation(out=tab[:, :, 1, 0:32], in_=frac[:, 0], func=ACT.Sin, scale=two_pi)
+            nc.scalar.activation(out=tab[:, :, 1, 32:64], in_=frac[:, 0], func=ACT.Sin, scale=-two_pi)
+            nc.scalar.activation(out=tab[:, :, 0, 0:32], in_=frac[:, 1], func=ACT.Sin, scale=two_pi)
+            nc.scalar.activation(out=tab[:, :, 0, 32:64], in_=frac[:, 1], func=ACT.Sin, scale=two_pi)
+
+        def first_pass(g):
+            for b in range(2):
+                for i in range(2):
+                    q_pass(i, b, g)
+
+        widen(0, 0)
+        turn(0, 0)
+        widen(0, 1)
+        turn(0, 1)
+        scale_quantize(0, 0)
+        first_pass(0)
+        widen(0, 2)
+        turn(0, 2)
+        scale_quantize(0, 1)
+        first_pass(1)
+        widen(0, 3)
+        turn(0, 3)
+        scale_quantize(0, 2)
+        first_pass(2)
+        tables()
+        widen(1, 0)
+        turn(1, 0)
+        scale_quantize(0, 3)
+        first_pass(3)
+        widen(1, 1)
+        turn(1, 1)
+        scale_quantize(1, 0)
+        q_group(0, 2)
+        widen(1, 2)
+        widen(1, 3)
+        q_finish(0, 0)
+        q_finish(1, 0)
+        turn(1, 2)
+        scale_quantize(1, 1)
+        q_group(1, 2)
+        q_finish(0, 1)
+        turn(1, 3)
+        scale_quantize(1, 2)
+        q_group(0, 3)
+        q_finish(1, 1)
+        scale_quantize(1, 3)
+        q_finish(0, 2)
+        q_store(0, 0)
+        q_group(1, 3)
+        q_finish(1, 2)
+        q_store(1, 0)
+        q_group(0, 4)
+        q_finish(0, 3)
+        q_group(1, 4)
+        q_finish(1, 3)
+        q_group(2, 0)
+        q_finish(0, 4)
+        q_group(3, 0)
+        q_finish(1, 4)
+        q_group(2, 1)
+        permute_latent()
+        q_finish(2, 0)
+        q_group(3, 1)
+        q_finish(3, 0)
+        q_group(2, 2)
+        q_finish(2, 1)
+        latent(0)
+        q_finish(3, 1)
+        latent(1)
+        latent_copy(0)
+        q_group(3, 2)
+        latent_copy(1)
+        q_finish(2, 2)
+        q_store(2, 0)
+        latent_quantize(0)
+        latent_quantize(1)
+        latent(2)
+        q_finish(3, 2)
+        q_store(3, 0)
+        latent(3)
+        latent_copy(2)
+        q_group(0, 5)
+        latent_copy(3)
+        latent_quantize(2)
+        latent_quantize(3)
+        k_up(0)
+        q_finish(0, 5)
+        q_store(0, 1)
+        q_group(1, 5)
+        up(0, "v", wv, 0, 512, NK)
+        k_finish(0)
+        k_up(1)
+        q_finish(1, 5)
+        q_store(1, 1)
+        v_finish(0)
+        q_group(2, 3)
+        up(1, "v", wv, 0, 512, NK)
+        k_finish(1)
+        q_group(2, 4)
+        q_finish(2, 3)
+        v_finish(1)
+        k_up(2)
+        q_group(2, 5)
+        q_finish(2, 4)
+        k_finish(2)
+        up(2, "v", wv, 0, 512, NK)
+        k_up(3)
+        q_finish(2, 5)
+        q_store(2, 1)
+        v_finish(2)
+        q_group(3, 5)
+        k_finish(3)
+        up(3, "v", wv, 0, 512, NK)
+        q_group(3, 4)
+        q_finish(3, 5)
+        q_store_block(3, 5)
+        v_finish(3)
+        q_group(3, 3)
+        q_finish(3, 4)
+        q_store_block(3, 4)
+        q_finish(3, 3)
+        q_store_block(3, 3)

@@ -50,8 +50,7 @@ def tile_multiheadlatentattentionwithgqafused_pa_w8_kernel(
     with ExitStack() as ctx:
         keep = ctx.enter_context(tc.tile_pool(name="keep", bufs=1))
         ring = ctx.enter_context(tc.tile_pool(name="ring", bufs=3))
-        ps_t = ctx.enter_context(tc.psum_pool(name="ps_t", bufs=2))
-        ps_a = ctx.enter_context(tc.psum_pool(name="ps_a", bufs=6))
+        psum = ctx.enter_context(tc.psum_pool(name="psum", bufs=1))
         ctx.enter_context(tc.manual_schedule())
 
         x_rows = x_bytes.rearrange("b s k -> (b s) k")
@@ -59,6 +58,14 @@ def tile_multiheadlatentattentionwithgqafused_pa_w8_kernel(
         k_rows = out_k.rearrange("b s h d -> (b s) (h d)")
         v_rows = out_v.rearrange("b s h d -> (b s) (h d)")
         wqkv = wqkv_words.rearrange("g p n t -> p g (n t)")
+
+        state = {"turn": [0, 1, 2], "acc": [3, 4, 5, 6, 7]}
+
+        def bank_of(kind):
+            n = state[kind].pop(0)
+            state[kind].append(n)
+            bank = psum.tile([P, BLK], F32, name=f"bank{n}", tag=f"bank{n}")
+            return bank
 
         ident = keep.tile([P, P], F32, name="ident")
         xb_first = keep.tile([P, 2, 512], U8, name="xb_first")
@@ -73,7 +80,8 @@ def tile_multiheadlatentattentionwithgqafused_pa_w8_kernel(
         wsc = keep.tile([P, NQ + LORA], U8, name="wsc", align_bytes=64)
         upsc = keep.tile([P, NK + NV], U8, name="upsc", align_bytes=64)
         w01 = [keep.tile([P, 2 * BLK], U32, name=f"w01_{g}", align_bytes=64) for g in range(GROUPS)]
-        wblk = {b: keep.tile([P, GROUPS, BLK], U32, name=f"w_{b}", align_bytes=64) for b in (2, 3, 4, 5)}
+        wb2 = keep.tile([P, GROUPS, BLK], U32, name="wb2", align_bytes=64)
+        w345 = [keep.tile([P, HALF], U32, name=f"w345_{g}", align_bytes=64) for g in range(GROUPS)]
         wlat_in = keep.tile([P, GROUPS, LORA], U32, name="wlat_in", align_bytes=64)
         wlat = keep.tile([P, GROUPS, LORA], U32, name="wlat", align_bytes=64)
         wlsc = keep.tile([P, LORA], U8, name="wlsc", align_bytes=64)
@@ -86,14 +94,22 @@ def tile_multiheadlatentattentionwithgqafused_pa_w8_kernel(
         k_out = [keep.tile([P, NK], F32, name=f"k_{i}") for i in range(TILES)]
         v_out = [keep.tile([P, NV], F32, name=f"v_{i}") for i in range(TILES)]
 
-        nc.vector.memset(wsc[:, 0 : 2 * BLK].bitcast(I32), 0)
-        nc.vector.memset(wsc[:, 2 * BLK :].bitcast(I32), 0)
+        nc.vector.memset(wsc[:, 0:HALF].bitcast(I32), 0)
+        nc.vector.memset(wsc[:, HALF:].bitcast(I32), 0)
         nc.vector.memset(upsc[:].bitcast(I32), 0)
         warm = keep.tile([P, 1], F32, name="warm")
         nc.vector.memset(warm[:], 0.0)
         warm_out = keep.tile([P, 1], F32, name="warm_out")
         nc.scalar.dma_start(out=xsc[:], in_=x_scale.rearrange("a b (g p u e) -> p (a b g) u e", p=P, u=2, e=2))
         nc.scalar.activation(out=warm_out[:], in_=warm[:], func=ACT.Sin)
+
+        idle = keep.tile([P, BLK], BF16, name="idle")
+        nc.vector.memset(idle[:], 0.0)
+        spare = psum.tile([P, BLK], F32, name="bank7", tag="bank7")
+
+        def keep_busy(count):
+            for rep in range(count):
+                nc.tensor.matmul(out=spare[:], lhsT=idle[:, 0:P], rhs=idle[:], start=True, stop=True)
 
         make_identity(nc, ident[:])
         pos = keep.tile([P, 2, 1], F32, name="pos")
@@ -116,34 +132,13 @@ def tile_multiheadlatentattentionwithgqafused_pa_w8_kernel(
             rows = x_rows[256 * pair : 256 * pair + 256, k0:k1]
             nc.sync.dma_start(out=tile[:], in_=rows.rearrange("(j p) k -> p j k", p=P))
 
-        def load_scales(c0, c1):
-            for quad in range(4):
-                nc.sync.dma_start(
-                    out=wsc[32 * quad : 32 * quad + 16, c0:c1].bitcast(I32),
-                    in_=wqkv_scales[:, 4 * quad : 4 * quad + 4, c0:c1].bitcast(I32),
-                )
-
-        def load_block(tile, c0):
+        def load_scales(quad, c0, c1):
             nc.sync.dma_start(
-                out=tile[:].bitcast(I32), in_=wqkv[:, :, 4 * c0 : 4 * (c0 + BLK)].bitcast(I32)
+                out=wsc[32 * quad : 32 * quad + 16, c0:c1].bitcast(I32),
+                in_=wqkv_scales[:, 4 * quad : 4 * quad + 4, c0:c1].bitcast(I32),
             )
 
-        def load_w01(g):
-            nc.sync.dma_start(out=w01[g][:].bitcast(I32), in_=wqkv[:, g, 0 : 8 * BLK].bitcast(I32))
-
-        load_x(0, xb_first, 0, 512)
-        load_scales(0, 2 * BLK)
-        load_x(0, xb_rest, 512, 2048)
-        for g in range(GROUPS):
-            load_w01(g)
-        load_x(1, xb_pair1, 0, 2048)
-        load_block(wblk[2], 2 * BLK)
-        load_scales(2 * BLK, NQ + LORA)
-        load_block(wblk[3], 3 * BLK)
-        load_block(wblk[4], 4 * BLK)
-        load_block(wlat_in, NQ)
-        load_block(wblk[5], 5 * BLK)
-        for quad in range(4):
+        def load_up_scales(quad):
             rows = slice(32 * quad, 32 * quad + 4)
             nc.sync.dma_start(
                 out=upsc[rows, 0:NK].bitcast(I32), in_=wk_scales[0, 4 * quad : 4 * quad + 4, :].bitcast(I32)
@@ -151,8 +146,44 @@ def tile_multiheadlatentattentionwithgqafused_pa_w8_kernel(
             nc.sync.dma_start(
                 out=upsc[rows, NK:].bitcast(I32), in_=wv_scales[0, 4 * quad : 4 * quad + 4, :].bitcast(I32)
             )
-        nc.sync.dma_start(out=wk[:].bitcast(I32), in_=wk_words[0].rearrange("p n t -> p (n t)").bitcast(I32))
-        nc.sync.dma_start(out=wv[:].bitcast(I32), in_=wv_words[0].rearrange("p n t -> p (n t)").bitcast(I32))
+
+        def load_up(tile, words):
+            nc.sync.dma_start(out=tile[:].bitcast(I32), in_=words[0].rearrange("p n t -> p (n t)").bitcast(I32))
+
+        def load_block(tile, c0):
+            nc.sync.dma_start(
+                out=tile[:].bitcast(I32), in_=wqkv[:, :, 4 * c0 : 4 * (c0 + BLK)].bitcast(I32)
+            )
+
+        def load_front(g):
+            nc.sync.dma_start(out=w01[g][:].bitcast(I32), in_=wqkv[:, g, 0 : 8 * BLK].bitcast(I32))
+
+        def load_back(g):
+            nc.sync.dma_start(out=w345[g][:].bitcast(I32), in_=wqkv[:, g, 4 * HALF : 8 * HALF].bitcast(I32))
+
+        load_x(0, xb_first, 0, 512)
+        load_x(0, xb_rest, 512, 2048)
+        for quad in range(4):
+            load_scales(quad, 0, HALF)
+        load_front(0)
+        load_front(1)
+        load_front(2)
+        load_x(1, xb_pair1, 0, 2048)
+        load_front(3)
+        load_scales(0, HALF, NQ + LORA)
+        load_block(wb2, 2 * BLK)
+        load_scales(1, HALF, NQ + LORA)
+        load_scales(2, HALF, NQ + LORA)
+        load_scales(3, HALF, NQ + LORA)
+        load_block(wlat_in, NQ)
+        load_up_scales(0)
+        load_up_scales(1)
+        load_up(wk, wk_words)
+        load_up_scales(2)
+        load_up_scales(3)
+        load_up(wv, wv_words)
+        for g in range(GROUPS):
+            load_back(g)
 
         def x_slices(pair, j, g):
             if pair == 1:
@@ -161,15 +192,18 @@ def tile_multiheadlatentattentionwithgqafused_pa_w8_kernel(
                 return xb_first[:, j, :], xw_first[:, j, :]
             return xb_rest[:, j, 512 * (g - 1) : 512 * g], xw_rest[:, j, 512 * (g - 1) : 512 * g]
 
-        def widen(pair, g):
+        def widen(pair, g, shared=False):
             for j in range(2):
                 src, dst = x_slices(pair, j, g)
-                nc.scalar.copy(out=dst, in_=src.bitcast(FP8))
+                if shared and j == 1:
+                    nc.vector.tensor_copy(out=dst, in_=src.bitcast(FP8))
+                else:
+                    nc.scalar.copy(out=dst, in_=src.bitcast(FP8))
 
         turned = {}
 
         def turn(pair, g):
-            bank = ps_t.tile([P, 2, 2, P], F32, name="bank", tag="bank")
+            bank = bank_of("turn")[:].rearrange("p (j u r) -> p j u r", j=2, u=2)
             for j in range(2):
                 words = x_slices(pair, j, g)[1].bitcast(F32)
                 for u in range(2):
@@ -202,11 +236,13 @@ def tile_multiheadlatentattentionwithgqafused_pa_w8_kernel(
         def w_slice(b, g):
             if b < 2:
                 return w01[g][:, BLK * b : BLK * b + BLK]
-            return wblk[b][:, g, :]
+            if b == 2:
+                return wb2[:, g, :]
+            return w345[g][:, BLK * (b - 3) : BLK * (b - 3) + BLK]
 
         def q_pass(i, b, g):
             if g == 0:
-                acc[i, b] = ps_a.tile([P, BLK], F32, name="acc", tag="acc")
+                acc[i, b] = bank_of("acc")
             rows = slice(P * i, P * i + P)
             nc.tensor.matmul_mx(
                 out=acc[i, b][:],
@@ -225,16 +261,16 @@ def tile_multiheadlatentattentionwithgqafused_pa_w8_kernel(
         def heads(ap):
             return ap.rearrange("p (h d) -> p h d", d=D_ROPE)
 
-        def rope(i, bank, dst, n):
+        def rope(i, bank, dst, n, adder, multiplier=nc.vector):
             prod = ring.tile([P, 2, 3, D_ROPE], F32, name="prod", tag="prod")
             a = i % 2
-            nc.vector.tensor_tensor(
+            multiplier.tensor_tensor(
                 out=prod[:, :, 0:n, :],
                 in0=bank.unsqueeze(1).broadcast_to([P, 2, n, D_ROPE]),
                 in1=tab[:, a].unsqueeze(2).broadcast_to([P, 2, n, D_ROPE]),
                 op=ALU.mult,
             )
-            nc.vector.tensor_tensor(
+            adder.tensor_tensor(
                 out=dst.rearrange("p h (k d) -> p h k d", k=2),
                 in0=prod[:, 0, 0:n, :].rearrange("p h (k d) -> p h k d", k=2),
                 in1=prod[:, 1, 0:n, :].rearrange("p h (k d) -> p h k d", k=2)[:, :, ::-1, :],
@@ -253,16 +289,54 @@ def tile_multiheadlatentattentionwithgqafused_pa_w8_kernel(
 
         LAYOUT = ((2, 0, slice(6, 8)), (0, 1, slice(7, 8)), (1, 2, slice(0, 1)))
 
-        def finish_512(i, bank, dst, kind):
+        def finish_512(i, bank, dst, kind, adder):
             r0, first, lone = LAYOUT[kind]
             src, to = heads(bank), heads(dst)
             n = len(range(r0, 8, 3))
-            rope(i, src[:, r0:8:3, :], to[:, r0:8:3, :], n)
+            rope(i, src[:, r0:8:3, :], to[:, r0:8:3, :], n, adder)
             plain(src, to, first, lone)
 
-        def q_finish(i, b):
+        def q_finish(i, b, adder=nc.gpsimd):
             c0 = BLK * (b % 3)
-            finish_512(i, acc[i, b][:], q_out[i, b // 3][:, c0 : c0 + BLK], b % 3)
+            finish_512(i, acc[i, b][:], q_out[i, b // 3][:, c0 : c0 + BLK], b % 3, adder)
+
+        def q_last(i, b):
+            rows = slice(P * i, P * i + P)
+            to = heads(q_out[i, b // 3][:, BLK * (b % 3) : BLK * (b % 3) + BLK])
+            for half in range(2):
+                bank = bank_of("acc")
+                cols = slice(256 * half, 256 * half + 256)
+                for g in range(GROUPS):
+                    nc.tensor.matmul_mx(
+                        out=bank[:, 0:256],
+                        lhsT=xq[:, g, rows].bitcast(FP8X4),
+                        lhsT_scale=xs[:, g, rows],
+                        rhs=w_slice(b, g)[:, cols].bitcast(FP8X4),
+                        rhs_scale=wsc[4 * g : P, BLK * b + 256 * half : BLK * b + 256 * half + 256],
+                        start=(g == 0),
+                        stop=(g == GROUPS - 1),
+                    )
+                src = heads(bank[:, 0:256])
+                dst = to[:, 4 * half : 4 * half + 4, :]
+                if half == 0:
+                    rope(i, src[:, 2:3, :], dst[:, 2:3, :], 1, nc.vector)
+                    nc.scalar.copy(out=dst[:, 0:2, :], in_=src[:, 0:2, :])
+                    nc.scalar.copy(out=dst[:, 3:4, :], in_=src[:, 3:4, :])
+                else:
+                    rope(i, src[:, 1:2, :], dst[:, 1:2, :], 1, nc.vector)
+                    nc.scalar.copy(out=dst[:, 2:4, :], in_=src[:, 2:4, :])
+                    nc.scalar.copy(out=dst[:, 0:1, :], in_=src[:, 0:1, :])
+                c0 = BLK * b + 256 * half
+                nc.sync.dma_start(
+                    out=q_rows[P * i : P * i + P, c0 : c0 + 256], in_=dst.rearrange("p h d -> p (h d)")
+                )
+
+        def q_finish_late(i, b):
+            to = q_out[i, b // 3][:, BLK * (b % 3) : BLK * (b % 3) + BLK]
+            nc.scalar.copy(out=to, in_=acc[i, b][:])
+            part = heads(to)[:, LAYOUT[b % 3][0] : 8 : 3, :]
+            n = part.shape[1]
+            rope(i, part, part, n, nc.gpsimd, nc.gpsimd)
 
         def q_store(i, h):
             nc.sync.dma_start(out=q_rows[P * i : P * i + P, HALF * h : HALF * h + HALF], in_=q_out[i, h][:])
@@ -283,40 +357,44 @@ def tile_multiheadlatentattentionwithgqafused_pa_w8_kernel(
                 in_=wsc[:, NQ:].rearrange("p (m t) -> p t m", t=4),
             )
 
-        def latent(i):
-            bank = ps_a.tile([P, BLK], F32, name="acc", tag="acc")
-            acc["lat", i] = bank
-            rows = slice(P * i, P * i + P)
-            for t in range(4):
-                cols = slice(P * t, P * t + P)
-                for g in range(GROUPS):
-                    nc.tensor.matmul_mx(
-                        out=bank[:, cols],
-                        lhsT=wlat[:, g, cols].bitcast(FP8X4),
-                        lhsT_scale=wlsc[4 * g : P, cols],
-                        rhs=xq[:, g, rows].bitcast(FP8X4),
-                        rhs_scale=xs[:, g, rows],
-                        start=(g == 0),
-                        stop=(g == GROUPS - 1),
-                    )
+        def latent(pair):
+            rows = slice(2 * P * pair, 2 * P * pair + 2 * P)
+            for half in range(2):
+                bank = bank_of("acc")
+                acc["lat", pair, half] = bank
+                for k in range(2):
+                    cols = slice(P * (2 * half + k), P * (2 * half + k) + P)
+                    for g in range(GROUPS):
+                        nc.tensor.matmul_mx(
+                            out=bank[:, 2 * P * k : 2 * P * k + 2 * P],
+                            lhsT=wlat[:, g, cols].bitcast(FP8X4),
+                            lhsT_scale=wlsc[4 * g : P, cols],
+                            rhs=xq[:, g, rows].bitcast(FP8X4),
+                            rhs_scale=xs[:, g, rows],
+                            start=(g == 0),
+                            stop=(g == GROUPS - 1),
+                        )
 
         ck_tiles = {}
 
-        def latent_copy(i):
-            ck = ring.tile([P, P, 4], BF16, name="ck", tag="ck", bufs=2, align_bytes=64)
-            nc.scalar.copy(out=ck[:], in_=acc["lat", i][:].rearrange("p (t r) -> p r t", t=4))
-            ck_tiles[i] = ck
+        def latent_copy(pair):
+            ck = ring.tile([P, 2 * P, 2, 2], BF16, name="ck", tag="ck", bufs=2, align_bytes=64)
+            for half in range(2):
+                nc.scalar.copy(
+                    out=ck[:, :, half, :], in_=acc["lat", pair, half][:].rearrange("p (k r) -> p r k", k=2)
+                )
+            ck_tiles[pair] = ck
 
-        def latent_quantize(i):
-            rows = slice(P * i, P * i + P)
+        def latent_quantize(pair):
+            rows = slice(2 * P * pair, 2 * P * pair + 2 * P)
             nc.vector.quantize_mx(
                 out=ckq[:, rows].bitcast(FP8X4),
                 scales=cks[:, rows],
-                in_=ck_tiles[i][:].rearrange("p r t -> p (r t)"),
+                in_=ck_tiles[pair][:].rearrange("p r h k -> p (r h k)"),
             )
 
         def up(i, key, words, c0, n, s0):
-            bank = ps_a.tile([P, BLK], F32, name="acc", tag="acc")
+            bank = bank_of("acc")
             acc[key, i] = bank
             rows = slice(P * i, P * i + P)
             nc.tensor.matmul_mx(
@@ -334,10 +412,10 @@ def tile_multiheadlatentattentionwithgqafused_pa_w8_kernel(
             up(i, "k1", wk, 512, 256, 512)
 
         def k_finish(i):
-            finish_512(i, acc["k0", i][:], k_out[i][:, 0:512], 0)
+            finish_512(i, acc["k0", i][:], k_out[i][:, 0:512], 0, nc.gpsimd)
             src = heads(acc["k1", i][:, 0:256])
             to = heads(k_out[i][:, 512:768])
-            rope(i, src[:, 0:4:3, :], to[:, 0:4:3, :], 2)
+            rope(i, src[:, 0:4:3, :], to[:, 0:4:3, :], 2, nc.gpsimd)
             nc.scalar.copy(out=to[:, 1:3, :], in_=src[:, 1:3, :])
             nc.sync.dma_start(out=k_rows[P * i : P * i + P, :], in_=k_out[i][:])
 
@@ -363,115 +441,129 @@ def tile_multiheadlatentattentionwithgqafused_pa_w8_kernel(
                 for i in range(2):
                     q_pass(i, b, g)
 
-        widen(0, 0)
+        g = nc.gpsimd
+        keep_busy(5)
+        widen(0, 0, True)
         turn(0, 0)
         widen(0, 1)
         turn(0, 1)
+        keep_busy(2)
         scale_quantize(0, 0)
         first_pass(0)
         widen(0, 2)
+        widen(0, 3)
         turn(0, 2)
         scale_quantize(0, 1)
-        first_pass(1)
-        widen(0, 3)
         turn(0, 3)
+        first_pass(1)
         scale_quantize(0, 2)
         first_pass(2)
-        tables()
         widen(1, 0)
+        widen(1, 1)
+        tables()
         turn(1, 0)
+        turn(1, 1)
         scale_quantize(0, 3)
         first_pass(3)
-        widen(1, 1)
-        turn(1, 1)
-        scale_quantize(1, 0)
-        q_group(0, 2)
         widen(1, 2)
         widen(1, 3)
-        q_finish(0, 0)
-        q_finish(1, 0)
-        turn(1, 2)
-        scale_quantize(1, 1)
-        q_group(1, 2)
-        q_finish(0, 1)
-        turn(1, 3)
-        scale_quantize(1, 2)
-        q_group(0, 3)
-        q_finish(1, 1)
-        scale_quantize(1, 3)
-        q_finish(0, 2)
-        q_store(0, 0)
-        q_group(1, 3)
-        q_finish(1, 2)
-        q_store(1, 0)
-        q_group(0, 4)
-        q_finish(0, 3)
-        q_group(1, 4)
-        q_finish(1, 3)
-        q_group(2, 0)
-        q_finish(0, 4)
-        q_group(3, 0)
-        q_finish(1, 4)
-        q_group(2, 1)
-        permute_latent()
-        q_finish(2, 0)
-        q_group(3, 1)
-        q_finish(3, 0)
-        q_group(2, 2)
-        q_finish(2, 1)
-        latent(0)
-        q_finish(3, 1)
-        latent(1)
-        latent_copy(0)
-        q_group(3, 2)
-        latent_copy(1)
-        q_finish(2, 2)
-        q_store(2, 0)
-        latent_quantize(0)
-        latent_quantize(1)
-        latent(2)
-        q_finish(3, 2)
-        q_store(3, 0)
-        latent(3)
-        latent_copy(2)
-        q_group(0, 5)
-        latent_copy(3)
-        latent_quantize(2)
-        latent_quantize(3)
-        k_up(0)
-        q_finish(0, 5)
-        q_store(0, 1)
-        q_group(1, 5)
-        up(0, "v", wv, 0, 512, NK)
-        k_finish(0)
-        k_up(1)
-        q_finish(1, 5)
-        q_store(1, 1)
-        v_finish(0)
-        q_group(2, 3)
-        up(1, "v", wv, 0, 512, NK)
-        k_finish(1)
-        q_group(2, 4)
-        q_finish(2, 3)
-        v_finish(1)
-        k_up(2)
-        q_group(2, 5)
-        q_finish(2, 4)
-        k_finish(2)
-        up(2, "v", wv, 0, 512, NK)
-        k_up(3)
-        q_finish(2, 5)
-        q_store(2, 1)
-        v_finish(2)
-        q_group(3, 5)
-        k_finish(3)
-        up(3, "v", wv, 0, 512, NK)
-        q_group(3, 4)
-        q_finish(3, 5)
-        q_store_block(3, 5)
-        v_finish(3)
-        q_group(3, 3)
-        q_finish(3, 4)
-        q_store_block(3, 4)
-        q_finish(3, 3)
-        q_store_block(3, 3)
+
+        done = set()
+        LATE = ((0, 0), (0, 1), (1, 0), (1, 1), (0, 2), (1, 2))
+
+        def start(kind, i, b):
+            if kind == "q":
+                q_group(i, b)
+            if kind == "lat":
+                latent(i)
+            if kind == "k":
+                k_up(i)
+            if kind == "v":
+                up(i, "v", wv, 0, 512, NK)
+
+        def finish(kind, i, b):
+            if kind == "q":
+                if (i, b) in LATE:
+                    q_finish_late(i, b)
+                else:
+                    q_finish(i, b)
+                done.add((i, b))
+                h = b // 3
+                if i == 3 and h == 1:
+                    q_store_block(i, b)
+                elif all((i, c) in done for c in range(3 * h, 3 * h + 3)):
+                    q_store(i, h)
+            if kind == "lat":
+                latent_copy(i)
+                quant_due.append(i)
+            if kind == "k":
+                k_finish(i)
+            if kind == "v":
+                v_finish(i)
+
+        ITEMS = [
+            ("x", 0, 0),
+            ("f", 0, 0),
+            ("q", 0, 2),
+            ("t", 2, 0),
+            ("t", 3, 0),
+            ("x", 1, 0),
+            ("f", 1, 0),
+            ("perm", 0, 0),
+            ("q", 1, 2),
+            ("f", 0, 1),
+            ("x", 2, 0),
+            ("f", 1, 1),
+            ("lat", 0, 0),
+            ("x", 3, 0),
+            ("acc", 0, 0),
+            ("q", 2, 0),
+            ("lat", 1, 0),
+            ("k", 0, 0),
+            ("v", 0, 0),
+            ("k", 1, 0),
+            ("v", 1, 0),
+            ("q", 2, 1),
+            ("q", 2, 2),
+            ("q", 3, 0),
+            ("q", 3, 1),
+            ("q", 3, 2),
+            ("k", 2, 0),
+            ("v", 2, 0),
+            ("q", 0, 3),
+            ("q", 0, 4),
+            ("q", 0, 5),
+            ("k", 3, 0),
+            ("v", 3, 0),
+            ("q", 1, 3),
+            ("q", 1, 4),
+            ("q", 1, 5),
+            ("q", 2, 3),
+            ("q", 2, 4),
+            ("q", 2, 5),
+            ("q", 3, 5),
+            ("q", 3, 4),
+        ]
+        waiting = []
+        quant_due = []
+        for kind, i, b in ITEMS:
+            if kind == "t":
+                turn(1, i)
+            elif kind == "x":
+                scale_quantize(1, i)
+            elif kind == "perm":
+                permute_latent()
+            elif kind == "f":
+                finish("q", i, b)
+            elif kind == "acc":
+                state["acc"].extend([0, 1, 2])
+            else:
+                while quant_due:
+                    latent_quantize(quant_due.pop(0))
+                start(kind, i, b)
+                for old in waiting:
+                    finish(*old)
+                waiting = [(kind, i, b)]
+        for old in waiting:
+            finish(*old)
+        q_last(3, 3)

@@ -59,20 +59,24 @@ def tile_multiheadlatentattentionwithgqafused_pa_w8_kernel(
         v_rows = out_v.rearrange("b s h d -> (b s) (h d)")
         wqkv = wqkv_words.rearrange("g p n t -> p g (n t)")
 
-        state = {"turn": [0, 1, 2], "acc": [3, 4, 5, 6, 7]}
+        free = list(range(8))
+        held = {}
 
-        def bank_of(kind):
-            n = state[kind].pop(0)
-            state[kind].append(n)
+        def bank_for(key):
+            n = free.pop(0)
             bank = psum.tile([P, BLK], F32, name=f"bank{n}", tag=f"bank{n}")
+            held[key] = n
             return bank
 
+        def release(key):
+            free.append(held.pop(key))
+
         ident = keep.tile([P, P], F32, name="ident")
-        xb_first = keep.tile([P, 2, 512], U8, name="xb_first")
-        xb_rest = keep.tile([P, 2, 1536], U8, name="xb_rest")
+        xb_first = keep.tile([P, 2, 1024], U8, name="xb_first")
+        xb_rest = keep.tile([P, 2, 1024], U8, name="xb_rest")
         xb_pair1 = keep.tile([P, 2, 2048], U8, name="xb_pair1")
-        xw_first = keep.tile([P, 2, 512], BF16, name="xw_first")
-        xw_rest = keep.tile([P, 2, 1536], BF16, name="xw_rest")
+        xw_first = keep.tile([P, 2, 1024], BF16, name="xw_first")
+        xw_rest = keep.tile([P, 2, 1024], BF16, name="xw_rest")
         xw_pair1 = keep.tile([P, 2, 2048], BF16, name="xw_pair1")
         xsc = keep.tile([P, GROUPS, 2, 2], F32, name="xsc")
         xq = keep.tile([P, GROUPS, TOK], U32, name="xq", align_bytes=64)
@@ -82,9 +86,7 @@ def tile_multiheadlatentattentionwithgqafused_pa_w8_kernel(
         w01 = [keep.tile([P, 2 * BLK], U32, name=f"w01_{g}", align_bytes=64) for g in range(GROUPS)]
         wb2 = keep.tile([P, GROUPS, BLK], U32, name="wb2", align_bytes=64)
         w345 = [keep.tile([P, HALF], U32, name=f"w345_{g}", align_bytes=64) for g in range(GROUPS)]
-        wlat_in = keep.tile([P, GROUPS, LORA], U32, name="wlat_in", align_bytes=64)
         wlat = keep.tile([P, GROUPS, LORA], U32, name="wlat", align_bytes=64)
-        wlsc = keep.tile([P, LORA], U8, name="wlsc", align_bytes=64)
         wk = keep.tile([P, NK], U32, name="wk", align_bytes=64)
         wv = keep.tile([P, NV], U32, name="wv", align_bytes=64)
         ckq = keep.tile([P, TOK], U32, name="ckq", align_bytes=64)
@@ -94,8 +96,8 @@ def tile_multiheadlatentattentionwithgqafused_pa_w8_kernel(
         k_out = [keep.tile([P, NK], F32, name=f"k_{i}") for i in range(TILES)]
         v_out = [keep.tile([P, NV], F32, name=f"v_{i}") for i in range(TILES)]
 
-        nc.vector.memset(wsc[:, 0:HALF].bitcast(I32), 0)
-        nc.vector.memset(wsc[:, HALF:].bitcast(I32), 0)
+        nc.vector.memset(wsc[:, 0 : 2 * BLK].bitcast(I32), 0)
+        nc.vector.memset(wsc[:, 2 * BLK :].bitcast(I32), 0)
         nc.vector.memset(upsc[:].bitcast(I32), 0)
         warm = keep.tile([P, 1], F32, name="warm")
         nc.vector.memset(warm[:], 0.0)
@@ -161,36 +163,65 @@ def tile_multiheadlatentattentionwithgqafused_pa_w8_kernel(
         def load_back(g):
             nc.sync.dma_start(out=w345[g][:].bitcast(I32), in_=wqkv[:, g, 4 * HALF : 8 * HALF].bitcast(I32))
 
-        load_x(0, xb_first, 0, 512)
-        load_x(0, xb_rest, 512, 2048)
-        for quad in range(4):
-            load_scales(quad, 0, HALF)
-        load_front(0)
-        load_front(1)
-        load_front(2)
-        load_x(1, xb_pair1, 0, 2048)
-        load_front(3)
-        load_scales(0, HALF, NQ + LORA)
-        load_block(wb2, 2 * BLK)
-        load_scales(1, HALF, NQ + LORA)
-        load_scales(2, HALF, NQ + LORA)
-        load_scales(3, HALF, NQ + LORA)
-        load_block(wlat_in, NQ)
-        load_up_scales(0)
-        load_up_scales(1)
-        load_up(wk, wk_words)
-        load_up_scales(2)
-        load_up_scales(3)
-        load_up(wv, wv_words)
-        for g in range(GROUPS):
-            load_back(g)
+        LOADS = [
+            ("x", 0),
+            ("sa", 0),
+            ("sb", 2),
+            ("x", 1),
+            ("f", 0),
+            ("sa", 3),
+            ("sa", 1),
+            ("sa", 2),
+            ("x", 2),
+            ("f", 1),
+            ("f", 2),
+            ("us", 1),
+            ("sb", 3),
+            ("f", 3),
+            ("sb", 0),
+            ("sb", 1),
+            ("b2", 0),
+            ("lat", 0),
+            ("b", 1),
+            ("wv", 0),
+            ("us", 3),
+            ("wk", 0),
+            ("b", 0),
+            ("us", 2),
+            ("us", 0),
+            ("b", 2),
+            ("b", 3),
+        ]
+        for kind, n in LOADS:
+            if kind == "x":
+                pair, tile, k0, k1 = ((0, xb_first, 0, 1024), (0, xb_rest, 1024, 2048), (1, xb_pair1, 0, 2048))[n]
+                load_x(pair, tile, k0, k1)
+            elif kind == "sa":
+                load_scales(n, 0, 2 * BLK)
+            elif kind == "sb":
+                load_scales(n, 2 * BLK, NQ + LORA)
+            elif kind == "f":
+                load_front(n)
+            elif kind == "b2":
+                load_block(wb2, 2 * BLK)
+            elif kind == "lat":
+                load_block(wlat, NQ)
+            elif kind == "us":
+                load_up_scales(n)
+            elif kind == "wk":
+                load_up(wk, wk_words)
+            elif kind == "wv":
+                load_up(wv, wv_words)
+            elif kind == "b":
+                load_back(n)
 
         def x_slices(pair, j, g):
             if pair == 1:
                 return xb_pair1[:, j, 512 * g : 512 * g + 512], xw_pair1[:, j, 512 * g : 512 * g + 512]
-            if g == 0:
-                return xb_first[:, j, :], xw_first[:, j, :]
-            return xb_rest[:, j, 512 * (g - 1) : 512 * g], xw_rest[:, j, 512 * (g - 1) : 512 * g]
+            cols = slice(512 * (g % 2), 512 * (g % 2) + 512)
+            if g < 2:
+                return xb_first[:, j, cols], xw_first[:, j, cols]
+            return xb_rest[:, j, cols], xw_rest[:, j, cols]
 
         def widen(pair, g, shared=False):
             for j in range(2):
@@ -203,7 +234,7 @@ def tile_multiheadlatentattentionwithgqafused_pa_w8_kernel(
         turned = {}
 
         def turn(pair, g):
-            bank = bank_of("turn")[:].rearrange("p (j u r) -> p j u r", j=2, u=2)
+            bank = bank_for(("x", pair, g))[:].rearrange("p (j u r) -> p j u r", j=2, u=2)
             for j in range(2):
                 words = x_slices(pair, j, g)[1].bitcast(F32)
                 for u in range(2):
@@ -223,6 +254,7 @@ def tile_multiheadlatentattentionwithgqafused_pa_w8_kernel(
                     op=ALU.mult,
                 )
                 parts.append(xt)
+            release(("x", pair, g))
             for j in range(2):
                 cols = slice(256 * pair + 128 * j, 256 * pair + 128 * j + 128)
                 nc.vector.quantize_mx(
@@ -242,7 +274,7 @@ def tile_multiheadlatentattentionwithgqafused_pa_w8_kernel(
 
         def q_pass(i, b, g):
             if g == 0:
-                acc[i, b] = bank_of("acc")
+                acc[i, b] = bank_for((i, b))
             rows = slice(P * i, P * i + P)
             nc.tensor.matmul_mx(
                 out=acc[i, b][:],
@@ -261,50 +293,82 @@ def tile_multiheadlatentattentionwithgqafused_pa_w8_kernel(
         def heads(ap):
             return ap.rearrange("p (h d) -> p h d", d=D_ROPE)
 
-        def rope(i, bank, dst, n, adder, multiplier=nc.vector):
-            prod = ring.tile([P, 2, 3, D_ROPE], F32, name="prod", tag="prod")
-            a = i % 2
-            multiplier.tensor_tensor(
-                out=prod[:, :, 0:n, :],
-                in0=bank.unsqueeze(1).broadcast_to([P, 2, n, D_ROPE]),
-                in1=tab[:, a].unsqueeze(2).broadcast_to([P, 2, n, D_ROPE]),
+        def multiply(i, part, prod, mul):
+            n = part.shape[1]
+            mul.tensor_tensor(
+                out=prod,
+                in0=part.unsqueeze(1).broadcast_to([P, 2, n, D_ROPE]),
+                in1=tab[:, i % 2].unsqueeze(2).broadcast_to([P, 2, n, D_ROPE]),
                 op=ALU.mult,
             )
-            adder.tensor_tensor(
-                out=dst.rearrange("p h (k d) -> p h k d", k=2),
-                in0=prod[:, 0, 0:n, :].rearrange("p h (k d) -> p h k d", k=2),
-                in1=prod[:, 1, 0:n, :].rearrange("p h (k d) -> p h k d", k=2)[:, :, ::-1, :],
+
+        def combine(prod, part, add):
+            add.tensor_tensor(
+                out=part.rearrange("p h (k d) -> p h k d", k=2),
+                in0=prod[:, 0].rearrange("p h (k d) -> p h k d", k=2),
+                in1=prod[:, 1].rearrange("p h (k d) -> p h k d", k=2)[:, :, ::-1, :],
                 op=ALU.add,
             )
 
-        def plain(bank, dst, first, lone):
-            for view in (bank, dst):
-                assert view.shape[1] == 8
+        def rope_parts(tile):
+            return tile[:].rearrange("p (h d) -> p h d", d=D_QK)[:, :, D_NOPE:D_QK]
+
+        LAYOUT = (
+            (2, 0, slice(6, 8), slice(0, 2)),
+            (0, 1, slice(7, 8), slice(2, 5)),
+            (1, 2, slice(0, 1), slice(5, 8)),
+        )
+
+        def finish_512(i, bank, dst, prod, kind):
+            r0, first, lone, hs = LAYOUT[kind]
+            src, to = heads(bank), heads(dst)
+            multiply(i, src[:, r0:8:3, :], prod[:, :, hs, :], nc.vector)
             pairs = slice(first, first + 6)
             nc.scalar.copy(
-                out=dst[:, pairs, :].rearrange("p (a c) d -> p a c d", c=3)[:, :, 0:2, :],
-                in_=bank[:, pairs, :].rearrange("p (a c) d -> p a c d", c=3)[:, :, 0:2, :],
+                out=to[:, pairs, :].rearrange("p (a c) d -> p a c d", c=3)[:, :, 0:2, :],
+                in_=src[:, pairs, :].rearrange("p (a c) d -> p a c d", c=3)[:, :, 0:2, :],
             )
-            nc.scalar.copy(out=dst[:, lone, :], in_=bank[:, lone, :])
+            nc.scalar.copy(out=to[:, lone, :], in_=src[:, lone, :])
 
-        LAYOUT = ((2, 0, slice(6, 8)), (0, 1, slice(7, 8)), (1, 2, slice(0, 1)))
+        def new_prod():
+            prod = ring.tile([P, 2, 8, D_ROPE], F32, name="prod", tag="prod", bufs=3)
+            return prod
 
-        def finish_512(i, bank, dst, kind, adder):
-            r0, first, lone = LAYOUT[kind]
-            src, to = heads(bank), heads(dst)
-            n = len(range(r0, 8, 3))
-            rope(i, src[:, r0:8:3, :], to[:, r0:8:3, :], n, adder)
-            plain(src, to, first, lone)
+        prods = {}
 
-        def q_finish(i, b, adder=nc.gpsimd):
+        def q_finish(i, b):
+            h = b // 3
+            if (i, h) not in prods:
+                prods[i, h] = keep.tile([P, 2, 8, D_ROPE], F32, name=f"prod_{i}_{h}")
             c0 = BLK * (b % 3)
-            finish_512(i, acc[i, b][:], q_out[i, b // 3][:, c0 : c0 + BLK], b % 3, adder)
+            finish_512(i, acc[i, b][:], q_out[i, h][:, c0 : c0 + BLK], prods[i, h], b % 3)
+            release((i, b))
+
+        def q_combine(i, h):
+            combine(prods[i, h], rope_parts(q_out[i, h]), nc.gpsimd)
+            q_store(i, h)
+
+        def q_combine_block(i, b):
+            h = b // 3
+            hs = LAYOUT[b % 3][3]
+            combine(prods[i, h][:, :, hs, :], rope_parts(q_out[i, h])[:, hs, :], nc.vector)
+            q_store_block(i, b)
+
+        def q_copy(i, b):
+            nc.scalar.copy(out=q_out[i, b // 3][:, BLK * (b % 3) : BLK * (b % 3) + BLK], in_=acc[i, b][:])
+            release((i, b))
+
+        def q_rotate(i, h):
+            prod = new_prod()
+            multiply(i, rope_parts(q_out[i, h]), prod[:], nc.gpsimd)
+            combine(prod, rope_parts(q_out[i, h]), nc.gpsimd)
+            q_store(i, h)
 
         def q_last(i, b):
             rows = slice(P * i, P * i + P)
             to = heads(q_out[i, b // 3][:, BLK * (b % 3) : BLK * (b % 3) + BLK])
             for half in range(2):
-                bank = bank_of("acc")
+                bank = bank_for((i, b, half))
                 cols = slice(256 * half, 256 * half + 256)
                 for g in range(GROUPS):
                     nc.tensor.matmul_mx(
@@ -318,25 +382,18 @@ def tile_multiheadlatentattentionwithgqafused_pa_w8_kernel(
                     )
                 src = heads(bank[:, 0:256])
                 dst = to[:, 4 * half : 4 * half + 4, :]
-                if half == 0:
-                    rope(i, src[:, 2:3, :], dst[:, 2:3, :], 1, nc.vector)
-                    nc.scalar.copy(out=dst[:, 0:2, :], in_=src[:, 0:2, :])
-                    nc.scalar.copy(out=dst[:, 3:4, :], in_=src[:, 3:4, :])
-                else:
-                    rope(i, src[:, 1:2, :], dst[:, 1:2, :], 1, nc.vector)
-                    nc.scalar.copy(out=dst[:, 2:4, :], in_=src[:, 2:4, :])
-                    nc.scalar.copy(out=dst[:, 0:1, :], in_=src[:, 0:1, :])
+                r0 = 2 - half
+                prod = prods[i, b // 3][:, :, half : half + 1, :]
+                multiply(i, src[:, r0 : r0 + 1, :], prod, nc.vector)
+                combine(prod, dst[:, r0 : r0 + 1, :], nc.vector)
+                pair = slice(2 * half, 2 * half + 2)
+                lone = slice(3 - 3 * half, 4 - 3 * half)
+                nc.scalar.copy(out=dst[:, pair, :], in_=src[:, pair, :])
+                nc.scalar.copy(out=dst[:, lone, :], in_=src[:, lone, :])
                 c0 = BLK * b + 256 * half
                 nc.sync.dma_start(
                     out=q_rows[P * i : P * i + P, c0 : c0 + 256], in_=dst.rearrange("p h d -> p (h d)")
                 )
-
-        def q_finish_late(i, b):
-            to = q_out[i, b // 3][:, BLK * (b % 3) : BLK * (b % 3) + BLK]
-            nc.scalar.copy(out=to, in_=acc[i, b][:])
-            part = heads(to)[:, LAYOUT[b % 3][0] : 8 : 3, :]
-            n = part.shape[1]
-            rope(i, part, part, n, nc.gpsimd, nc.gpsimd)
 
         def q_store(i, h):
             nc.sync.dma_start(out=q_rows[P * i : P * i + P, HALF * h : HALF * h + HALF], in_=q_out[i, h][:])
@@ -347,54 +404,60 @@ def tile_multiheadlatentattentionwithgqafused_pa_w8_kernel(
                 out=q_rows[P * i : P * i + P, BLK * b : BLK * b + BLK], in_=q_out[i, b // 3][:, c0 : c0 + BLK]
             )
 
-        def permute_latent():
-            nc.vector.tensor_copy(
-                out=wlat[:].bitcast(I32).rearrange("p g (t m) -> p g t m", t=4),
-                in_=wlat_in[:].bitcast(I32).rearrange("p g (m t) -> p g t m", t=4),
-            )
-            nc.vector.tensor_copy(
-                out=wlsc[:].rearrange("p (t m) -> p t m", t=4),
-                in_=wsc[:, NQ:].rearrange("p (m t) -> p t m", t=4),
-            )
+        def latent(i):
+            bank = bank_for(("lat", i))
+            acc["lat", i] = bank
+            rows = slice(P * i, P * i + P)
+            for g in range(GROUPS):
+                nc.tensor.matmul_mx(
+                    out=bank[:],
+                    lhsT=xq[:, g, rows].bitcast(FP8X4),
+                    lhsT_scale=xs[:, g, rows],
+                    rhs=wlat[:, g, :].bitcast(FP8X4),
+                    rhs_scale=wsc[4 * g : P, NQ : NQ + LORA],
+                    start=(g == 0),
+                    stop=(g == GROUPS - 1),
+                )
 
-        def latent(pair):
-            rows = slice(2 * P * pair, 2 * P * pair + 2 * P)
-            for half in range(2):
-                bank = bank_of("acc")
-                acc["lat", pair, half] = bank
-                for k in range(2):
-                    cols = slice(P * (2 * half + k), P * (2 * half + k) + P)
-                    for g in range(GROUPS):
-                        nc.tensor.matmul_mx(
-                            out=bank[:, 2 * P * k : 2 * P * k + 2 * P],
-                            lhsT=wlat[:, g, cols].bitcast(FP8X4),
-                            lhsT_scale=wlsc[4 * g : P, cols],
-                            rhs=xq[:, g, rows].bitcast(FP8X4),
-                            rhs_scale=xs[:, g, rows],
-                            start=(g == 0),
-                            stop=(g == GROUPS - 1),
-                        )
+        ck_rows = {}
+
+        def latent_copy(i):
+            ckr = ring.tile([P, 2, P, 2], BF16, name="ckr", tag="ckr", bufs=4)
+            nc.scalar.copy(out=ckr[:], in_=acc["lat", i][:].rearrange("p (m u e) -> p u m e", u=2, e=2))
+            ck_rows[i] = ckr
+            release(("lat", i))
+
+        ck_banks = {}
+
+        def latent_turn(pair):
+            bank = bank_for(("ck", pair))[:].rearrange("p (j u r) -> p j u r", j=2, u=2)
+            for j in range(2):
+                words = ck_rows[2 * pair + j][:].rearrange("p u m e -> p u (m e)").bitcast(F32)
+                for u in range(2):
+                    nc.tensor.transpose(bank[:, j, u, :], words[:, u, :], ident[:])
+            ck_banks[pair] = bank
 
         ck_tiles = {}
 
-        def latent_copy(pair):
-            ck = ring.tile([P, 2 * P, 2, 2], BF16, name="ck", tag="ck", bufs=2, align_bytes=64)
-            for half in range(2):
-                nc.scalar.copy(
-                    out=ck[:, :, half, :], in_=acc["lat", pair, half][:].rearrange("p (k r) -> p r k", k=2)
-                )
+        def latent_spread(pair):
+            ck = ring.tile([P, 2, P, 4], BF16, name="ck", tag="ck", bufs=2, align_bytes=64)
+            nc.scalar.copy(
+                out=ck[:].rearrange("p j r t -> p j (r t)").bitcast(F32).rearrange("p j (r u) -> p j r u", u=2),
+                in_=ck_banks[pair].rearrange("p j u r -> p j r u"),
+            )
             ck_tiles[pair] = ck
+            release(("ck", pair))
 
         def latent_quantize(pair):
             rows = slice(2 * P * pair, 2 * P * pair + 2 * P)
             nc.vector.quantize_mx(
                 out=ckq[:, rows].bitcast(FP8X4),
                 scales=cks[:, rows],
-                in_=ck_tiles[pair][:].rearrange("p r h k -> p (r h k)"),
+                in_=ck_tiles[pair][:].rearrange("p j r t -> p (j r t)"),
             )
 
         def up(i, key, words, c0, n, s0):
-            bank = bank_of("acc")
+            bank = bank_for((key, i))
             acc[key, i] = bank
             rows = slice(P * i, P * i + P)
             nc.tensor.matmul_mx(
@@ -412,15 +475,19 @@ def tile_multiheadlatentattentionwithgqafused_pa_w8_kernel(
             up(i, "k1", wk, 512, 256, 512)
 
         def k_finish(i):
-            finish_512(i, acc["k0", i][:], k_out[i][:, 0:512], 0, nc.gpsimd)
+            prod = new_prod()
+            finish_512(i, acc["k0", i][:], k_out[i][:, 0:512], prod, 0)
             src = heads(acc["k1", i][:, 0:256])
-            to = heads(k_out[i][:, 512:768])
-            rope(i, src[:, 0:4:3, :], to[:, 0:4:3, :], 2, nc.gpsimd)
-            nc.scalar.copy(out=to[:, 1:3, :], in_=src[:, 1:3, :])
+            multiply(i, src[:, 0:4:3, :], prod[:, :, 2:4, :], nc.vector)
+            nc.scalar.copy(out=heads(k_out[i][:, 512:768])[:, 1:3, :], in_=src[:, 1:3, :])
+            release(("k0", i))
+            release(("k1", i))
+            combine(prod[:, :, 0:4, :], rope_parts(k_out[i]), nc.gpsimd)
             nc.sync.dma_start(out=k_rows[P * i : P * i + P, :], in_=k_out[i][:])
 
         def v_finish(i):
             nc.scalar.copy(out=v_out[i][:], in_=acc["v", i][:])
+            release(("v", i))
             nc.sync.dma_start(out=v_rows[P * i : P * i + P, :], in_=v_out[i][:])
 
         def tables():
@@ -441,35 +508,9 @@ def tile_multiheadlatentattentionwithgqafused_pa_w8_kernel(
                 for i in range(2):
                     q_pass(i, b, g)
 
-        g = nc.gpsimd
-        keep_busy(5)
-        widen(0, 0, True)
-        turn(0, 0)
-        widen(0, 1)
-        turn(0, 1)
-        keep_busy(2)
-        scale_quantize(0, 0)
-        first_pass(0)
-        widen(0, 2)
-        widen(0, 3)
-        turn(0, 2)
-        scale_quantize(0, 1)
-        turn(0, 3)
-        first_pass(1)
-        scale_quantize(0, 2)
-        first_pass(2)
-        widen(1, 0)
-        widen(1, 1)
-        tables()
-        turn(1, 0)
-        turn(1, 1)
-        scale_quantize(0, 3)
-        first_pass(3)
-        widen(1, 2)
-        widen(1, 3)
 
         done = set()
-        LATE = ((0, 0), (0, 1), (1, 0), (1, 1), (0, 2), (1, 2))
+        LATER = ((0, 0), (1, 0))
 
         def start(kind, i, b):
             if kind == "q":
@@ -483,83 +524,123 @@ def tile_multiheadlatentattentionwithgqafused_pa_w8_kernel(
 
         def finish(kind, i, b):
             if kind == "q":
-                if (i, b) in LATE:
-                    q_finish_late(i, b)
+                h = b // 3
+                if (i, h) in LATER:
+                    q_copy(i, b)
                 else:
                     q_finish(i, b)
-                done.add((i, b))
-                h = b // 3
-                if i == 3 and h == 1:
-                    q_store_block(i, b)
-                elif all((i, c) in done for c in range(3 * h, 3 * h + 3)):
-                    q_store(i, h)
+                    done.add((i, b))
+                    if (i, h) == (3, 1):
+                        q_combine_block(i, b)
+                    elif all((i, c) in done for c in range(3 * h, 3 * h + 3)):
+                        q_combine(i, h)
             if kind == "lat":
                 latent_copy(i)
-                quant_due.append(i)
             if kind == "k":
                 k_finish(i)
             if kind == "v":
                 v_finish(i)
 
         ITEMS = [
-            ("x", 0, 0),
-            ("f", 0, 0),
-            ("q", 0, 2),
+            ("w", 0, 1),
+            ("busy", 5, 0),
+            ("w", 1, 1),
+            ("t", 0, 0),
+            ("t", 1, 0),
+            ("w", 2, 0),
             ("t", 2, 0),
-            ("t", 3, 0),
+            ("w", 3, 0),
+            ("w", 4, 0),
+            ("w", 7, 0),
+            ("x", 0, 0),
+            ("w", 6, 0),
             ("x", 1, 0),
-            ("f", 1, 0),
-            ("perm", 0, 0),
-            ("q", 1, 2),
-            ("f", 0, 1),
             ("x", 2, 0),
-            ("f", 1, 1),
-            ("lat", 0, 0),
+            ("A", 0, 0),
+            ("w", 5, 0),
+            ("t", 3, 0),
+            ("t", 4, 0),
             ("x", 3, 0),
-            ("acc", 0, 0),
-            ("q", 2, 0),
+            ("A", 1, 0),
+            ("tab", 0, 0),
+            ("A", 2, 0),
+            ("A", 3, 0),
+            ("f", 0, 1),
+            ("t", 6, 0),
+            ("t", 5, 0),
+            ("x", 4, 0),
+            ("x", 6, 0),
+            ("t", 7, 0),
+            ("f", 1, 1),
+            ("q", 0, 2),
+            ("x", 5, 0),
+            ("q", 1, 2),
+            ("lat", 0, 0),
+            ("f", 0, 0),
             ("lat", 1, 0),
-            ("k", 0, 0),
+            ("x", 7, 0),
+            ("q", 2, 0),
+            ("ct", 0, 0),
+            ("lat", 2, 0),
+            ("q", 3, 0),
+            ("cs", 0, 0),
+            ("cq", 0, 0),
+            ("lat", 3, 0),
+            ("q", 2, 2),
+            ("f", 1, 0),
+            ("r", 0, 0),
             ("v", 0, 0),
             ("k", 1, 0),
-            ("v", 1, 0),
-            ("q", 2, 1),
-            ("q", 2, 2),
-            ("q", 3, 0),
-            ("q", 3, 1),
-            ("q", 3, 2),
-            ("k", 2, 0),
-            ("v", 2, 0),
+            ("r", 1, 0),
             ("q", 0, 3),
-            ("q", 0, 4),
+            ("ct", 1, 0),
             ("q", 0, 5),
-            ("k", 3, 0),
+            ("cs", 1, 0),
+            ("k", 0, 0),
+            ("q", 2, 1),
+            ("q", 3, 2),
+            ("cq", 1, 0),
+            ("v", 1, 0),
+            ("q", 3, 1),
+            ("k", 2, 0),
+            ("q", 2, 4),
+            ("v", 2, 0),
             ("v", 3, 0),
+            ("q", 0, 4),
             ("q", 1, 3),
+            ("k", 3, 0),
             ("q", 1, 4),
             ("q", 1, 5),
-            ("q", 2, 3),
-            ("q", 2, 4),
             ("q", 2, 5),
+            ("q", 2, 3),
             ("q", 3, 5),
             ("q", 3, 4),
         ]
         waiting = []
-        quant_due = []
         for kind, i, b in ITEMS:
             if kind == "t":
-                turn(1, i)
+                turn(i // 4, i % 4)
             elif kind == "x":
-                scale_quantize(1, i)
-            elif kind == "perm":
-                permute_latent()
+                scale_quantize(i // 4, i % 4)
+            elif kind == "w":
+                widen(i // 4, i % 4, b == 1)
+            elif kind == "A":
+                first_pass(i)
+            elif kind == "busy":
+                keep_busy(i)
+            elif kind == "tab":
+                tables()
+            elif kind == "ct":
+                latent_turn(i)
+            elif kind == "cs":
+                latent_spread(i)
+            elif kind == "cq":
+                latent_quantize(i)
+            elif kind == "r":
+                q_rotate(i, b)
             elif kind == "f":
                 finish("q", i, b)
-            elif kind == "acc":
-                state["acc"].extend([0, 1, 2])
             else:
-                while quant_due:
-                    latent_quantize(quant_due.pop(0))
                 start(kind, i, b)
                 for old in waiting:
                     finish(*old)

import math
from contextlib import ExitStack

import concourse.mybir as mybir
from concourse.masks import make_identity

B, S, HID = 2, 256, 2048
NH, NKV, LORA = 16, 4, 512
D_NOPE, D_ROPE, D_V = 128, 64, 128
D_QK = D_NOPE + D_ROPE
NQ = NH * D_QK
NK = NKV * D_QK
NV = NKV * D_V
TOK = B * S

FLOPS = 2 * TOK * HID * (NQ + LORA) + 2 * TOK * LORA * (NK + NV)

F32 = mybir.dt.float32
BF16 = mybir.dt.bfloat16
I32 = mybir.dt.int32
U32 = mybir.dt.uint32
U8 = mybir.dt.uint8
FP8 = mybir.dt.float8_e4m3fn
FP8X4 = mybir.dt.float8_e4m3fn_x4
ALU = mybir.AluOpType
ACT = mybir.ActivationFunctionType

P = 128
GROUPS = HID // 512
BLK = 512
HALF = 3 * BLK
TILES = TOK // P


def tile_multiheadlatentattentionwithgqafused_pa_w8_kernel(
    tc,
    x_bytes,
    x_scale,
    wqkv_words,
    wqkv_scales,
    wk_words,
    wk_scales,
    wv_words,
    wv_scales,
    out_q,
    out_k,
    out_v,
):
    nc = tc.nc
    with ExitStack() as ctx:
        keep = ctx.enter_context(tc.tile_pool(name="keep", bufs=1))
        ring = ctx.enter_context(tc.tile_pool(name="ring", bufs=3))
        psum = ctx.enter_context(tc.psum_pool(name="psum", bufs=1))
        ctx.enter_context(tc.manual_schedule())

        x_rows = x_bytes.rearrange("b s k -> (b s) k")
        q_rows = out_q.rearrange("b s h d -> (b s) (h d)")
        k_rows = out_k.rearrange("b s h d -> (b s) (h d)")
        v_rows = out_v.rearrange("b s h d -> (b s) (h d)")
        wqkv = wqkv_words.rearrange("g p n t -> p g (n t)")

        free = list(range(8))
        held = {}

        def bank_for(key):
            n = free.pop(0)
            bank = psum.tile([P, BLK], F32, name=f"bank{n}", tag=f"bank{n}")
            held[key] = n
            return bank

        def release(key):
            free.append(held.pop(key))

        ident = keep.tile([P, P], F32, name="ident")
        xb_first = keep.tile([P, 2, 1024], U8, name="xb_first")
        xb_rest = keep.tile([P, 2, 1024], U8, name="xb_rest")
        xb_pair1 = keep.tile([P, 2, 2048], U8, name="xb_pair1")
        xw_first = keep.tile([P, 2, 1024], BF16, name="xw_first")
        xw_rest = keep.tile([P, 2, 1024], BF16, name="xw_rest")
        xw_pair1 = keep.tile([P, 2, 2048], BF16, name="xw_pair1")
        xsc = keep.tile([P, GROUPS, 2, 2], F32, name="xsc")
        xq = keep.tile([P, GROUPS, TOK], U32, name="xq", align_bytes=64)
        xs = keep.tile([P, GROUPS, TOK], U8, name="xs", align_bytes=64)
        wsc = keep.tile([P, NQ + LORA], U8, name="wsc", align_bytes=64)
        upsc = keep.tile([P, NK + NV], U8, name="upsc", align_bytes=64)
        w01 = [keep.tile([P, 2 * BLK], U32, name=f"w01_{g}", align_bytes=64) for g in range(GROUPS)]
        wb2 = keep.tile([P, GROUPS, BLK], U32, name="wb2", align_bytes=64)
        w345 = [keep.tile([P, HALF], U32, name=f"w345_{g}", align_bytes=64) for g in range(GROUPS)]
        wlat = keep.tile([P, GROUPS, LORA], U32, name="wlat", align_bytes=64)
        wk = keep.tile([P, NK], U32, name="wk", align_bytes=64)
        wv = keep.tile([P, NV], U32, name="wv", align_bytes=64)
        ckq = keep.tile([P, TOK], U32, name="ckq", align_bytes=64)
        cks = keep.tile([P, TOK], U8, name="cks", align_bytes=64)
        tab = keep.tile([P, 2, 2, D_ROPE], F32, name="tab")
        q_out = {(i, h): keep.tile([P, HALF], F32, name=f"q_{i}_{h}") for i in range(TILES) for h in range(2)}
        k_out = [keep.tile([P, NK], F32, name=f"k_{i}") for i in range(TILES)]
        v_out = [keep.tile([P, NV], F32, name=f"v_{i}") for i in range(TILES)]

        nc.vector.memset(wsc[:, 0 : 2 * BLK].bitcast(I32), 0)
        nc.vector.memset(wsc[:, 2 * BLK :].bitcast(I32), 0)
        nc.vector.memset(upsc[:].bitcast(I32), 0)
        warm = keep.tile([P, 1], F32, name="warm")
        nc.vector.memset(warm[:], 0.0)
        warm_out = keep.tile([P, 1], F32, name="warm_out")
        nc.scalar.dma_start(out=xsc[:], in_=x_scale.rearrange("a b (g p u e) -> p (a b g) u e", p=P, u=2, e=2))
        nc.scalar.activation(out=warm_out[:], in_=warm[:], func=ACT.Sin)

        idle = keep.tile([P, BLK], BF16, name="idle")
        nc.vector.memset(idle[:], 0.0)
        spare = psum.tile([P, BLK], F32, name="bank7", tag="bank7")

        def keep_busy(count):
            for rep in range(count):
                nc.tensor.matmul(out=spare[:], lhsT=idle[:, 0:P], rhs=idle[:], start=True, stop=True)

        make_identity(nc, ident[:])
        pos = keep.tile([P, 2, 1], F32, name="pos")
        nc.gpsimd.iota(pos[:], [[P, 2], [0, 1]], base=0, channel_multiplier=1, allow_small_or_imprecise_dtypes=True)
        ang = keep.tile([P, 2, 2, 32], F32, name="ang")
        nc.gpsimd.tensor_scalar(
            out=ang[:, 0, :, 0:1], in0=pos[:], scalar1=1.0 / (2.0 * math.pi), scalar2=None, op0=ALU.mult
        )
        for m in (1, 2, 4, 8, 16):
            nc.gpsimd.tensor_scalar(
                out=ang[:, 0, :, m : 2 * m],
                in0=ang[:, 0, :, 0:m],
                scalar1=10000.0 ** (-m / 32.0),
                scalar2=None,
                op0=ALU.mult,
            )
        nc.gpsimd.tensor_scalar(out=ang[:, 1], in0=ang[:, 0], scalar1=0.25, scalar2=None, op0=ALU.add)

        def load_x(pair, tile, k0, k1):
            rows = x_rows[256 * pair : 256 * pair + 256, k0:k1]
            nc.sync.dma_start(out=tile[:], in_=rows.rearrange("(j p) k -> p j k", p=P))

        def load_scales(quad, c0, c1):
            nc.sync.dma_start(
                out=wsc[32 * quad : 32 * quad + 16, c0:c1].bitcast(I32),
                in_=wqkv_scales[:, 4 * quad : 4 * quad + 4, c0:c1].bitcast(I32),
            )

        def load_up_scales(quad):
            rows = slice(32 * quad, 32 * quad + 4)
            nc.sync.dma_start(
                out=upsc[rows, 0:NK].bitcast(I32), in_=wk_scales[0, 4 * quad : 4 * quad + 4, :].bitcast(I32)
            )
            nc.sync.dma_start(
                out=upsc[rows, NK:].bitcast(I32), in_=wv_scales[0, 4 * quad : 4 * quad + 4, :].bitcast(I32)
            )

        def load_up(tile, words):
            nc.sync.dma_start(out=tile[:].bitcast(I32), in_=words[0].rearrange("p n t -> p (n t)").bitcast(I32))

        def load_block(tile, c0):
            nc.sync.dma_start(
                out=tile[:].bitcast(I32), in_=wqkv[:, :, 4 * c0 : 4 * (c0 + BLK)].bitcast(I32)
            )

        def load_front(g):
            nc.sync.dma_start(out=w01[g][:].bitcast(I32), in_=wqkv[:, g, 0 : 8 * BLK].bitcast(I32))

        def load_back(g):
            nc.sync.dma_start(out=w345[g][:].bitcast(I32), in_=wqkv[:, g, 4 * HALF : 8 * HALF].bitcast(I32))

        LOADS = [
            ("x", 0),
            ("sa", 0),
            ("sb", 2),
            ("x", 1),
            ("f", 0),
            ("sa", 3),
            ("sa", 1),
            ("sa", 2),
            ("x", 2),
            ("f", 1),
            ("f", 2),
            ("us", 1),
            ("sb", 3),
            ("f", 3),
            ("sb", 0),
            ("sb", 1),
            ("b2", 0),
            ("lat", 0),
            ("b", 1),
            ("wv", 0),
            ("us", 3),
            ("wk", 0),
            ("b", 0),
            ("us", 2),
            ("us", 0),
            ("b", 2),
            ("b", 3),
        ]
        for kind, n in LOADS:
            if kind == "x":
                pair, tile, k0, k1 = ((0, xb_first, 0, 1024), (0, xb_rest, 1024, 2048), (1, xb_pair1, 0, 2048))[n]
                load_x(pair, tile, k0, k1)
            elif kind == "sa":
                load_scales(n, 0, 2 * BLK)
            elif kind == "sb":
                load_scales(n, 2 * BLK, NQ + LORA)
            elif kind == "f":
                load_front(n)
            elif kind == "b2":
                load_block(wb2, 2 * BLK)
            elif kind == "lat":
                load_block(wlat, NQ)
            elif kind == "us":
                load_up_scales(n)
            elif kind == "wk":
                load_up(wk, wk_words)
            elif kind == "wv":
                load_up(wv, wv_words)
            elif kind == "b":
                load_back(n)

        def x_slices(pair, j, g):
            if pair == 1:
                return xb_pair1[:, j, 512 * g : 512 * g + 512], xw_pair1[:, j, 512 * g : 512 * g + 512]
            cols = slice(512 * (g % 2), 512 * (g % 2) + 512)
            if g < 2:
                return xb_first[:, j, cols], xw_first[:, j, cols]
            return xb_rest[:, j, cols], xw_rest[:, j, cols]

        def widen(pair, g, shared=False):
            for j in range(2):
                src, dst = x_slices(pair, j, g)
                if shared and j == 1:
                    nc.vector.tensor_copy(out=dst, in_=src.bitcast(FP8))
                else:
                    nc.scalar.copy(out=dst, in_=src.bitcast(FP8))

        turned = {}

        def turn(pair, g):
            bank = bank_for(("x", pair, g))[:].rearrange("p (j u r) -> p j u r", j=2, u=2)
            for j in range(2):
                words = x_slices(pair, j, g)[1].bitcast(F32)
                for u in range(2):
                    nc.tensor.transpose(bank[:, j, u, :], words[:, u:256:2], ident[:])
            turned[pair, g] = bank

        def scale_quantize(pair, g):
            bank = turned[pair, g]
            parts = []
            for j in range(2):
                xt = ring.tile([P, P, 2, 2], BF16, name="xt", tag="xt", bufs=4, align_bytes=64)
                src = bank[:, j].rearrange("p u r -> p (u r)").bitcast(BF16)
                nc.vector.tensor_tensor(
                    out=xt[:],
                    in0=src.rearrange("p (u r e) -> p r u e", u=2, e=2),
                    in1=xsc[:, g].unsqueeze(1).broadcast_to([P, P, 2, 2]),
                    op=ALU.mult,
                )
                parts.append(xt)
            release(("x", pair, g))
            for j in range(2):
                cols = slice(256 * pair + 128 * j, 256 * pair + 128 * j + 128)
                nc.vector.quantize_mx(
                    out=xq[:, g, cols].bitcast(FP8X4),
                    scales=xs[:, g, cols],
                    in_=parts[j][:].rearrange("p r u e -> p (r u e)"),
                )

        acc = {}

        def w_slice(b, g):
            if b < 2:
                return w01[g][:, BLK * b : BLK * b + BLK]
            if b == 2:
                return wb2[:, g, :]
            return w345[g][:, BLK * (b - 3) : BLK * (b - 3) + BLK]

        def q_pass(i, b, g):
            if g == 0:
                acc[i, b] = bank_for((i, b))
            rows = slice(P * i, P * i + P)
            nc.tensor.matmul_mx(
                out=acc[i, b][:],
                lhsT=xq[:, g, rows].bitcast(FP8X4),
                lhsT_scale=xs[:, g, rows],
                rhs=w_slice(b, g).bitcast(FP8X4),
                rhs_scale=wsc[4 * g : P, BLK * b : BLK * b + BLK],
                start=(g == 0),
                stop=(g == GROUPS - 1),
            )

        def q_group(i, b):
            for g in range(GROUPS):
                q_pass(i, b, g)

        def heads(ap):
            return ap.rearrange("p (h d) -> p h d", d=D_ROPE)

        def multiply(i, part, prod, mul):
            n = part.shape[1]
            mul.tensor_tensor(
                out=prod,
                in0=part.unsqueeze(1).broadcast_to([P, 2, n, D_ROPE]),
                in1=tab[:, i % 2].unsqueeze(2).broadcast_to([P, 2, n, D_ROPE]),
                op=ALU.mult,
            )

        def combine(prod, part, add):
            add.tensor_tensor(
                out=part.rearrange("p h (k d) -> p h k d", k=2),
                in0=prod[:, 0].rearrange("p h (k d) -> p h k d", k=2),
                in1=prod[:, 1].rearrange("p h (k d) -> p h k d", k=2)[:, :, ::-1, :],
                op=ALU.add,
            )

        def rope_parts(tile):
            return tile[:].rearrange("p (h d) -> p h d", d=D_QK)[:, :, D_NOPE:D_QK]

        LAYOUT = (
            (2, 0, slice(6, 8), slice(0, 2)),
            (0, 1, slice(7, 8), slice(2, 5)),
            (1, 2, slice(0, 1), slice(5, 8)),
        )

        def finish_512(i, bank, dst, prod, kind):
            r0, first, lone, hs = LAYOUT[kind]
            src, to = heads(bank), heads(dst)
            multiply(i, src[:, r0:8:3, :], prod[:, :, hs, :], nc.vector)
            pairs = slice(first, first + 6)
            nc.scalar.copy(
                out=to[:, pairs, :].rearrange("p (a c) d -> p a c d", c=3)[:, :, 0:2, :],
                in_=src[:, pairs, :].rearrange("p (a c) d -> p a c d", c=3)[:, :, 0:2, :],
            )
            nc.scalar.copy(out=to[:, lone, :], in_=src[:, lone, :])

        def new_prod():
            prod = ring.tile([P, 2, 8, D_ROPE], F32, name="prod", tag="prod", bufs=3)
            return prod

        prods = {}

        def q_finish(i, b):
            h = b // 3
            if (i, h) not in prods:
                prods[i, h] = keep.tile([P, 2, 8, D_ROPE], F32, name=f"prod_{i}_{h}")
            c0 = BLK * (b % 3)
            finish_512(i, acc[i, b][:], q_out[i, h][:, c0 : c0 + BLK], prods[i, h], b % 3)
            release((i, b))

        def q_combine(i, h):
            combine(prods[i, h], rope_parts(q_out[i, h]), nc.gpsimd)
            q_store(i, h)

        def q_combine_block(i, b):
            h = b // 3
            hs = LAYOUT[b % 3][3]
            combine(prods[i, h][:, :, hs, :], rope_parts(q_out[i, h])[:, hs, :], nc.vector)
            q_store_block(i, b)

        def q_copy(i, b):
            nc.scalar.copy(out=q_out[i, b // 3][:, BLK * (b % 3) : BLK * (b % 3) + BLK], in_=acc[i, b][:])
            release((i, b))

        def q_rotate(i, h):
            prod = new_prod()
            multiply(i, rope_parts(q_out[i, h]), prod[:], nc.gpsimd)
            combine(prod, rope_parts(q_out[i, h]), nc.gpsimd)
            q_store(i, h)

        def q_last(i, b):
            rows = slice(P * i, P * i + P)
            to = heads(q_out[i, b // 3][:, BLK * (b % 3) : BLK * (b % 3) + BLK])
            for half in range(2):
                bank = bank_for((i, b, half))
                cols = slice(256 * half, 256 * half + 256)
                for g in range(GROUPS):
                    nc.tensor.matmul_mx(
                        out=bank[:, 0:256],
                        lhsT=xq[:, g, rows].bitcast(FP8X4),
                        lhsT_scale=xs[:, g, rows],
                        rhs=w_slice(b, g)[:, cols].bitcast(FP8X4),
                        rhs_scale=wsc[4 * g : P, BLK * b + 256 * half : BLK * b + 256 * half + 256],
                        start=(g == 0),
                        stop=(g == GROUPS - 1),
                    )
                src = heads(bank[:, 0:256])
                dst = to[:, 4 * half : 4 * half + 4, :]
                r0 = 2 - half
                prod = prods[i, b // 3][:, :, half : half + 1, :]
                multiply(i, src[:, r0 : r0 + 1, :], prod, nc.vector)
                combine(prod, dst[:, r0 : r0 + 1, :], nc.vector)
                pair = slice(2 * half, 2 * half + 2)
                lone = slice(3 - 3 * half, 4 - 3 * half)
                nc.scalar.copy(out=dst[:, pair, :], in_=src[:, pair, :])
                nc.scalar.copy(out=dst[:, lone, :], in_=src[:, lone, :])
                c0 = BLK * b + 256 * half
                nc.sync.dma_start(
                    out=q_rows[P * i : P * i + P, c0 : c0 + 256], in_=dst.rearrange("p h d -> p (h d)")
                )

        def q_store(i, h):
            nc.sync.dma_start(out=q_rows[P * i : P * i + P, HALF * h : HALF * h + HALF], in_=q_out[i, h][:])

        def q_store_block(i, b):
            c0 = BLK * (b % 3)
            nc.sync.dma_start(
                out=q_rows[P * i : P * i + P, BLK * b : BLK * b + BLK], in_=q_out[i, b // 3][:, c0 : c0 + BLK]
            )

        def latent(i):
            bank = bank_for(("lat", i))
            acc["lat", i] = bank
            rows = slice(P * i, P * i + P)
            for g in range(GROUPS):
                nc.tensor.matmul_mx(
                    out=bank[:],
                    lhsT=xq[:, g, rows].bitcast(FP8X4),
                    lhsT_scale=xs[:, g, rows],
                    rhs=wlat[:, g, :].bitcast(FP8X4),
                    rhs_scale=wsc[4 * g : P, NQ : NQ + LORA],
                    start=(g == 0),
                    stop=(g == GROUPS - 1),
                )

        ck_rows = {}

        def latent_copy(i):
            ckr = ring.tile([P, 2, P, 2], BF16, name="ckr", tag="ckr", bufs=4)
            nc.scalar.copy(out=ckr[:], in_=acc["lat", i][:].rearrange("p (m u e) -> p u m e", u=2, e=2))
            ck_rows[i] = ckr
            release(("lat", i))

        ck_banks = {}

        def latent_turn(pair):
            bank = bank_for(("ck", pair))[:].rearrange("p (j u r) -> p j u r", j=2, u=2)
            for j in range(2):
                words = ck_rows[2 * pair + j][:].rearrange("p u m e -> p u (m e)").bitcast(F32)
                for u in range(2):
                    nc.tensor.transpose(bank[:, j, u, :], words[:, u, :], ident[:])
            ck_banks[pair] = bank

        ck_tiles = {}

        def latent_spread(pair):
            ck = ring.tile([P, 2, P, 4], BF16, name="ck", tag="ck", bufs=2, align_bytes=64)
            nc.scalar.copy(
                out=ck[:].rearrange("p j r t -> p j (r t)").bitcast(F32).rearrange("p j (r u) -> p j r u", u=2),
                in_=ck_banks[pair].rearrange("p j u r -> p j r u"),
            )
            ck_tiles[pair] = ck
            release(("ck", pair))

        def latent_quantize(pair):
            rows = slice(2 * P * pair, 2 * P * pair + 2 * P)
            nc.vector.quantize_mx(
                out=ckq[:, rows].bitcast(FP8X4),
                scales=cks[:, rows],
                in_=ck_tiles[pair][:].rearrange("p j r t -> p (j r t)"),
            )

        def up(i, key, words, c0, n, s0):
            bank = bank_for((key, i))
            acc[key, i] = bank
            rows = slice(P * i, P * i + P)
            nc.tensor.matmul_mx(
                out=bank[:, 0:n],
                lhsT=ckq[:, rows].bitcast(FP8X4),
                lhsT_scale=cks[:, rows],
                rhs=words[:, c0 : c0 + n].bitcast(FP8X4),
                rhs_scale=upsc[:, s0 : s0 + n],
                start=True,
                stop=True,
            )

        def k_up(i):
            up(i, "k0", wk, 0, 512, 0)
            up(i, "k1", wk, 512, 256, 512)

        def k_finish(i):
            prod = new_prod()
            finish_512(i, acc["k0", i][:], k_out[i][:, 0:512], prod, 0)
            src = heads(acc["k1", i][:, 0:256])
            multiply(i, src[:, 0:4:3, :], prod[:, :, 2:4, :], nc.vector)
            nc.scalar.copy(out=heads(k_out[i][:, 512:768])[:, 1:3, :], in_=src[:, 1:3, :])
            release(("k0", i))
            release(("k1", i))
            combine(prod[:, :, 0:4, :], rope_parts(k_out[i]), nc.gpsimd)
            nc.sync.dma_start(out=k_rows[P * i : P * i + P, :], in_=k_out[i][:])

        def v_finish(i):
            nc.scalar.copy(out=v_out[i][:], in_=acc["v", i][:])
            release(("v", i))
            nc.sync.dma_start(out=v_rows[P * i : P * i + P, :], in_=v_out[i][:])

        def tables():
            whole = keep.tile([P, 2, 2, 32], I32, name="whole")
            nc.vector.tensor_copy(out=whole[:], in_=ang[:])
            turns = keep.tile([P, 2, 2, 32], F32, name="turns")
            nc.vector.tensor_copy(out=turns[:], in_=whole[:])
            frac = keep.tile([P, 2, 2, 32], F32, name="frac")
            nc.vector.tensor_tensor(out=frac[:], in0=ang[:], in1=turns[:], op=ALU.subtract)
            two_pi = 2.0 * math.pi
            nc.scalar.activation(out=tab[:, :, 1, 0:32], in_=frac[:, 0], func=ACT.Sin, scale=two_pi)
            nc.scalar.activation(out=tab[:, :, 1, 32:64], in_=frac[:, 0], func=ACT.Sin, scale=-two_pi)
            nc.scalar.activation(out=tab[:, :, 0, 0:32], in_=frac[:, 1], func=ACT.Sin, scale=two_pi)
            nc.scalar.activation(out=tab[:, :, 0, 32:64], in_=frac[:, 1], func=ACT.Sin, scale=two_pi)

        def first_pass(g):
            for b in range(2):
                for i in range(2):
                    q_pass(i, b, g)


        done = set()
        LATER = ((0, 0), (1, 0))

        def start(kind, i, b):
            if kind == "q":
                q_group(i, b)
            if kind == "lat":
                latent(i)
            if kind == "k":
                k_up(i)
            if kind == "v":
                up(i, "v", wv, 0, 512, NK)

        def finish(kind, i, b):
            if kind == "q":
                h = b // 3
                if (i, h) in LATER:
                    q_copy(i, b)
                else:
                    q_finish(i, b)
                    done.add((i, b))
                    if (i, h) == (3, 1):
                        q_combine_block(i, b)
                    elif all((i, c) in done for c in range(3 * h, 3 * h + 3)):
                        q_combine(i, h)
            if kind == "lat":
                latent_copy(i)
            if kind == "k":
                k_finish(i)
            if kind == "v":
                v_finish(i)

        ITEMS = [
            ("w", 0, 1),
            ("busy", 5, 0),
            ("w", 1, 1),
            ("t", 0, 0),
            ("t", 1, 0),
            ("w", 2, 0),
            ("t", 2, 0),
            ("w", 3, 0),
            ("w", 4, 0),
            ("w", 7, 0),
            ("x", 0, 0),
            ("w", 6, 0),
            ("x", 1, 0),
            ("x", 2, 0),
            ("A", 0, 0),
            ("w", 5, 0),
            ("t", 3, 0),
            ("t", 4, 0),
            ("x", 3, 0),
            ("A", 1, 0),
            ("tab", 0, 0),
            ("A", 2, 0),
            ("A", 3, 0),
            ("f", 0, 1),
            ("t", 6, 0),
            ("t", 5, 0),
            ("x", 4, 0),
            ("x", 6, 0),
            ("t", 7, 0),
            ("f", 1, 1),
            ("q", 0, 2),
            ("x", 5, 0),
            ("q", 1, 2),
            ("lat", 0, 0),
            ("f", 0, 0),
            ("lat", 1, 0),
            ("x", 7, 0),
            ("q", 2, 0),
            ("ct", 0, 0),
            ("lat", 2, 0),
            ("q", 3, 0),
            ("cs", 0, 0),
            ("cq", 0, 0),
            ("lat", 3, 0),
            ("q", 2, 2),
            ("f", 1, 0),
            ("r", 0, 0),
            ("v", 0, 0),
            ("k", 1, 0),
            ("r", 1, 0),
            ("q", 0, 3),
            ("ct", 1, 0),
            ("q", 0, 5),
            ("cs", 1, 0),
            ("k", 0, 0),
            ("q", 2, 1),
            ("q", 3, 2),
            ("cq", 1, 0),
            ("v", 1, 0),
            ("q", 3, 1),
            ("k", 2, 0),
            ("q", 2, 4),
            ("v", 2, 0),
            ("v", 3, 0),
            ("q", 0, 4),
            ("q", 1, 3),
            ("k", 3, 0),
            ("q", 1, 4),
            ("q", 1, 5),
            ("q", 2, 5),
            ("q", 2, 3),
            ("q", 3, 5),
            ("q", 3, 4),
        ]
        waiting = []
        for kind, i, b in ITEMS:
            if kind == "t":
                turn(i // 4, i % 4)
            elif kind == "x":
                scale_quantize(i // 4, i % 4)
            elif kind == "w":
                widen(i // 4, i % 4, b == 1)
            elif kind == "A":
                first_pass(i)
            elif kind == "busy":
                keep_busy(i)
            elif kind == "tab":
                tables()
            elif kind == "ct":
                latent_turn(i)
            elif kind == "cs":
                latent_spread(i)
            elif kind == "cq":
                latent_quantize(i)
            elif kind == "r":
                q_rotate(i, b)
            elif kind == "f":
                finish("q", i, b)
            else:
                start(kind, i, b)
                for old in waiting:
                    finish(*old)
                waiting = [(kind, i, b)]
        for old in waiting:
            finish(*old)
        q_last(3, 3)
